import numpy as np
import ml_dtypes


def mxq(x, axis, fmt="e4m3"):
    dtype, down = {"e4m3": (ml_dtypes.float8_e4m3fn, 7), "e5m2": (ml_dtypes.float8_e5m2, 14)}[fmt]
    v = np.moveaxis(np.asarray(x, np.float32).astype(ml_dtypes.bfloat16).astype(np.float64), axis, -1)
    blocks = v.reshape(v.shape[:-1] + (-1, 32))
    amax = np.abs(blocks).max(-1, keepdims=True)
    byte = np.maximum(np.where(amax > 0, np.frexp(amax)[1] - 1 + 127, 0) - down, 1)
    scale = np.exp2(byte - 127.0)
    codes = (blocks / scale).astype(np.float32).astype(dtype).astype(np.float64)
    return np.moveaxis((codes * scale).reshape(v.shape), -1, axis)


WIDE = False


def mx_kscale(k):
    if not WIDE:
        return np.ones(k)
    levels = np.array([10, -10, 5, -5, 0])
    a = np.random.permutation(np.resize(levels, k // 512 * 4)).reshape(k // 512, 4)
    idx = np.arange(k)
    return np.exp2(a[idx // 512, idx % 128 // 32])


BF16 = ml_dtypes.bfloat16


def bf(x):
    return np.asarray(x, np.float32).astype(BF16)


def f64(x):
    return np.asarray(x).astype(np.float64)


B, S, K, D, H, KV, HD = 2, 16, 32, 2048, 8, 2, 128
HP = HD // 2


def rope(v, cos, sin):
    vr, vi = v[..., 0::2], v[..., 1::2]
    out_r = vr * cos - vi * sin
    out_i = vr * sin + vi * cos
    return np.stack([out_r, out_i], axis=-1).reshape(v.shape)


def setup_inputs():
    s = mx_kscale(D)
    return {"x": bf(np.random.standard_normal((B, S, K, D)) * s),
            "freqs": bf(np.random.uniform(size=(S, K, HP)) * 2.0 * np.pi),
            "wq": bf(np.random.standard_normal((H * HD, D)) * 1.25 / np.sqrt(D) / s),
            "wk": bf(np.random.standard_normal((KV * HD, D)) * 1.25 / np.sqrt(D) / s),
            "wv": bf(np.random.standard_normal((KV * HD, D)) * 2.0 / np.sqrt(D) / s)}


def reference(x, freqs, wq, wk, wv):
    xm = mxq(f64(x), 3, "e4m3")
    q = (xm @ mxq(f64(wq), 1, "e4m3").T).reshape(B, S, K, H, HD)
    k = (xm @ mxq(f64(wk), 1, "e4m3").T).reshape(B, S, K, KV, HD)
    v = (xm @ mxq(f64(wv), 1, "e4m3").T).reshape(B, S, K, KV, HD)
    cos = np.cos(f64(freqs))[None, :, :, None, :]
    sin = np.sin(f64(freqs))[None, :, :, None, :]
    return rope(q, cos, sin), rope(k, cos, sin), v

@@ -1,0 +1,233 @@
+from contextlib import ExitStack
+
+import concourse.mybir as mybir
+from concourse.masks import make_identity
+
+F32 = mybir.dt.float32
+BF16 = mybir.dt.bfloat16
+U32 = mybir.dt.uint32
+U8 = mybir.dt.uint8
+FP8X4 = mybir.dt.float8_e4m3fn_x4
+MULT = mybir.AluOpType.mult
+ADD = mybir.AluOpType.add
+SIN = mybir.ActivationFunctionType.Sin
+
+P = 128
+PACK = 4
+K_PASS = P * PACK
+FEATURES = 2048
+PASSES = FEATURES // K_PASS
+WORDS = FEATURES // 2
+TOKENS = 2 * 16 * 32
+TOKEN_TILES = TOKENS // P
+POSITIONS = 16 * 32
+POSITION_TILES = POSITIONS // P
+HEAD = 128
+PAIRS = HEAD // 2
+Q_WIDTH = 8 * HEAD
+KV_WIDTH = 2 * HEAD
+CHUNK = 512
+CHUNK_BLOCKS = CHUNK // P
+CHUNKS = (Q_WIDTH + 2 * KV_WIDTH) // CHUNK
+X_AHEAD = 2
+
+FLOPS = 2 * TOKENS * FEATURES * (Q_WIDTH + 2 * KV_WIDTH)
+
+
+def blocks_after(chunk, tile):
+    blocks = []
+    if chunk == 0 and tile + X_AHEAD < TOKEN_TILES:
+        blocks.append(("x", tile + X_AHEAD))
+    if chunk + 1 < CHUNKS and tile < CHUNK_BLOCKS:
+        blocks.append(("w", (chunk + 1) * CHUNK_BLOCKS + tile))
+    return blocks
+
+
+def tile_attention_pa_kernel(tc, x, freqs, wq, wk, wv, out_0, out_1, out_2):
+    nc = tc.nc
+    x_rows = x.rearrange("b s k d -> (b s k) d")
+    angle_rows = freqs.rearrange("s k i -> (s k) i")
+    q_rows = out_0.rearrange("b s k h d -> (b s k) (h d)")
+    k_rows = out_1.rearrange("b s k h d -> (b s k) (h d)")
+    v_rows = out_2.rearrange("b s k h d -> (b s k) (h d)")
+
+    w_block_rows = (
+        [wq[r : r + P, :] for r in range(0, Q_WIDTH, P)]
+        + [wk[r : r + P, :] for r in range(0, KV_WIDTH, P)]
+        + [wv[r : r + P, :] for r in range(0, KV_WIDTH, P)]
+    )
+
+    with ExitStack() as ctx:
+        ctx.enter_context(tc.manual_schedule())
+
+        raw = ctx.enter_context(tc.tile_pool(name="raw", bufs=1))
+        tables = ctx.enter_context(tc.tile_pool(name="tables", bufs=1))
+        quantised = ctx.enter_context(tc.tile_pool(name="quantised", bufs=1))
+        x_stage = ctx.enter_context(tc.tile_pool(name="x_stage", bufs=3))
+        w_stage = ctx.enter_context(tc.tile_pool(name="w_stage", bufs=2))
+        work = ctx.enter_context(tc.tile_pool(name="work", bufs=3))
+        results = ctx.enter_context(tc.tile_pool(name="results", bufs=8))
+        turned = ctx.enter_context(tc.psum_pool(name="turned", bufs=4))
+        sums = ctx.enter_context(tc.psum_pool(name="sums", bufs=4))
+
+        x_raw = [raw.tile([P, FEATURES], BF16, name="x_raw%d" % t) for t in range(TOKEN_TILES)]
+        w_raw = [raw.tile([P, FEATURES], BF16, name="w_raw%d" % b) for b in range(CHUNKS * CHUNK_BLOCKS)]
+
+        def load(block):
+            kind, index = block
+            if kind == "x":
+                nc.sync.dma_start(out=x_raw[index][:], in_=x_rows[index * P : (index + 1) * P, :])
+            else:
+                nc.sync.dma_start(out=w_raw[index][:], in_=w_block_rows[index])
+
+        first_blocks = [("w", b) for b in range(CHUNK_BLOCKS)] + [("x", t) for t in range(X_AHEAD)]
+        for block in first_blocks:
+            load(block)
+        for chunk in range(CHUNKS):
+            for tile in range(TOKEN_TILES):
+                for block in blocks_after(chunk, tile):
+                    load(block)
+
+        angles = tables.tile([P, POSITION_TILES, PAIRS], BF16)
+        nc.scalar.dma_start(out=angles[:], in_=angle_rows.rearrange("(t p) i -> p t i", p=P))
+        identity = tables.tile([P, P], F32)
+        make_identity(nc, identity[:])
+
+        n_angles = POSITION_TILES * PAIRS
+        sin_half = tables.tile([P, n_angles], F32)
+        sin_quarter = tables.tile([P, n_angles], F32)
+        nc.scalar.activation(out=sin_half[:], in_=angles[:].rearrange("p t i -> p (t i)"), func=SIN, scale=0.5)
+        nc.scalar.activation(out=sin_quarter[:], in_=angles[:].rearrange("p t i -> p (t i)"), func=SIN, scale=0.25)
+
+        square_half = tables.tile([P, n_angles], F32)
+        cos_twice = tables.tile([P, POSITION_TILES, HEAD], F32)
+        nc.vector.tensor_tensor(out=square_half[:], in0=sin_half[:], in1=sin_half[:], op=MULT)
+        nc.vector.tensor_scalar(
+            out=cos_twice[:].rearrange("p t (i e) -> p (t i) e", e=2),
+            in0=square_half[:].unsqueeze(2).to_broadcast([P, n_angles, 2]),
+            scalar1=-2.0,
+            scalar2=1.0,
+            op0=MULT,
+            op1=ADD,
+        )
+        square_quarter = tables.tile([P, n_angles], F32)
+        cos_half = tables.tile([P, n_angles], F32)
+        half_sin = tables.tile([P, n_angles], F32)
+        signed_sin = tables.tile([P, POSITION_TILES, 2, PAIRS], F32)
+        nc.vector.tensor_tensor(out=square_quarter[:], in0=sin_quarter[:], in1=sin_quarter[:], op=MULT)
+        nc.vector.tensor_scalar(
+            out=cos_half[:], in0=square_quarter[:], scalar1=-2.0, scalar2=1.0, op0=MULT, op1=ADD
+        )
+        nc.vector.tensor_tensor(out=half_sin[:], in0=sin_half[:], in1=cos_half[:], op=MULT)
+        for e, factor in ((0, -2.0), (1, 2.0)):
+            nc.vector.tensor_scalar_mul(
+                out=signed_sin[:, :, e, :],
+                in0=half_sin[:].rearrange("p (t i) -> p t i", i=PAIRS),
+                scalar1=factor,
+            )
+
+        x_codes = [quantised.tile([P, PASSES * P], U32, name="x_codes%d" % t, align_bytes=64) for t in range(TOKEN_TILES)]
+        x_scales = [quantised.tile([P, PASSES * P], U8, name="x_scales%d" % t, align_bytes=64) for t in range(TOKEN_TILES)]
+        w_codes = [quantised.tile([P, PASSES, CHUNK], U32, name="w_codes%d" % c, align_bytes=64) for c in range(CHUNKS)]
+        w_scales = [quantised.tile([P, PASSES, CHUNK], U8, name="w_scales%d" % c, align_bytes=64) for c in range(CHUNKS)]
+        w_grouped = {}
+
+        def transpose_block(rows, grouped_words):
+            words = rows[:].bitcast(F32)
+            for first_pass in range(0, PASSES, 2):
+                bank = turned.tile([P, 2, 2, P], F32)
+                for g in range(2):
+                    for u in range(2):
+                        first_word = (2 * (first_pass + g) + u) * P
+                        nc.tensor.transpose(bank[:, g, u, :], words[:, first_word : first_word + P], identity[:])
+                nc.scalar.copy(
+                    out=grouped_words[:, first_pass : first_pass + 2, :, :],
+                    in_=bank[:].rearrange("p g u r -> p g r u"),
+                )
+
+        def prepare(block):
+            kind, index = block
+            if kind == "x":
+                grouped = x_stage.tile([P, PASSES * P * PACK], BF16, align_bytes=64)
+                transpose_block(
+                    x_raw[index], grouped[:].bitcast(F32).rearrange("p (g r u) -> p g r u", g=PASSES, u=2)
+                )
+                nc.vector.quantize_mx(
+                    out=x_codes[index][:].bitcast(FP8X4), scales=x_scales[index][:], in_=grouped[:]
+                )
+                return
+            chunk, place = divmod(index, CHUNK_BLOCKS)
+            if place == 0:
+                w_grouped[chunk] = w_stage.tile([P, PASSES * CHUNK * PACK], BF16, name="w_grouped", align_bytes=64)
+            grouped = w_grouped[chunk]
+            grouped_words = grouped[:].bitcast(F32).rearrange("p (g r u) -> p g r u", g=PASSES, u=2)
+            transpose_block(w_raw[index], grouped_words[:, :, place * P : (place + 1) * P, :])
+            if place == CHUNK_BLOCKS - 1:
+                for g in range(PASSES):
+                    nc.vector.quantize_mx(
+                        out=w_codes[chunk][:, g, :].bitcast(FP8X4),
+                        scales=w_scales[chunk][:, g, :],
+                        in_=grouped[:, g * CHUNK * PACK : (g + 1) * CHUNK * PACK],
+                    )
+
+        def project(tile, chunk, first_row, width):
+            total = sums.tile([P, width], F32, name="total")
+            for g in range(PASSES):
+                nc.tensor.matmul_mx(
+                    out=total[:],
+                    lhsT=x_codes[tile][:, g * P : (g + 1) * P].bitcast(FP8X4),
+                    lhsT_scale=x_scales[tile][:, g * P : (g + 1) * P],
+                    rhs=w_codes[chunk][:, g, first_row : first_row + width].bitcast(FP8X4),
+                    rhs_scale=w_scales[chunk][:, g, first_row : first_row + width],
+                    start=(g == 0),
+                    stop=(g == PASSES - 1),
+                )
+            return total
+
+        def rotate(total, tile, width):
+            heads = width // HEAD
+            t = tile % POSITION_TILES
+            by_cos = work.tile([P, width], F32, name="by_cos")
+            nc.vector.tensor_tensor(
+                out=by_cos[:].rearrange("p (h c) -> p h c", h=heads),
+                in0=total[:].rearrange("p (h c) -> p h c", h=heads),
+                in1=cos_twice[:, t, :].unsqueeze(1).to_broadcast([P, heads, HEAD]),
+                op=MULT,
+            )
+            by_sin = work.tile([P, 2, heads * PAIRS], F32, name="by_sin")
+            features = total[:].rearrange("p (h i e) -> p e h i", h=heads, e=2)
+            for e in range(2):
+                nc.vector.tensor_tensor(
+                    out=by_sin[:, e, :].rearrange("p (h i) -> p h i", h=heads),
+                    in0=features[:, 1 - e, :, :],
+                    in1=signed_sin[:, t, e, :].unsqueeze(1).to_broadcast([P, heads, PAIRS]),
+                    op=MULT,
+                )
+            rotated = results.tile([P, width], F32, name="rotated")
+            nc.vector.tensor_tensor(
+                out=rotated[:].rearrange("p (c e) -> p c e", e=2),
+                in0=by_cos[:].rearrange("p (c e) -> p c e", e=2),
+                in1=by_sin[:].rearrange("p e c -> p c e"),
+                op=ADD,
+            )
+            return rotated
+
+        for block in first_blocks:
+            prepare(block)
+        for chunk in range(CHUNKS):
+            for tile in range(TOKEN_TILES):
+                tokens = slice(tile * P, (tile + 1) * P)
+                if chunk * CHUNK < Q_WIDTH:
+                    total = project(tile, chunk, 0, CHUNK)
+                    rotated = rotate(total, tile, CHUNK)
+                    nc.sync.dma_start(out=q_rows[tokens, chunk * CHUNK : (chunk + 1) * CHUNK], in_=rotated[:])
+                else:
+                    k_total = project(tile, chunk, 0, KV_WIDTH)
+                    v_total = project(tile, chunk, KV_WIDTH, KV_WIDTH)
+                    k_rotated = rotate(k_total, tile, KV_WIDTH)
+                    nc.sync.dma_start(out=k_rows[tokens, :], in_=k_rotated[:])
+                    v_copy = results.tile([P, KV_WIDTH], F32)
+                    nc.scalar.copy(out=v_copy[:], in_=v_total[:])
+                    nc.sync.dma_start(out=v_rows[tokens, :], in_=v_copy[:])
+                for block in blocks_after(chunk, tile):
+                    prepare(block)

@@ -64,9 +64,9 @@ def tile_attention_pa_kernel(tc, x, freqs, wq, wk, wv, out_0, out_1, out_2):
         tables = ctx.enter_context(tc.tile_pool(name="tables", bufs=1))
         quantised = ctx.enter_context(tc.tile_pool(name="quantised", bufs=1))
         x_stage = ctx.enter_context(tc.tile_pool(name="x_stage", bufs=3))
-        w_stage = ctx.enter_context(tc.tile_pool(name="w_stage", bufs=2))
-        work = ctx.enter_context(tc.tile_pool(name="work", bufs=3))
-        results = ctx.enter_context(tc.tile_pool(name="results", bufs=8))
+        w_stage = ctx.enter_context(tc.tile_pool(name="w_stage", bufs=1))
+        work = ctx.enter_context(tc.tile_pool(name="work", bufs=6))
+        results = ctx.enter_context(tc.tile_pool(name="results", bufs=6))
         turned = ctx.enter_context(tc.psum_pool(name="turned", bufs=4))
         sums = ctx.enter_context(tc.psum_pool(name="sums", bufs=4))
 
@@ -204,7 +204,7 @@ def tile_attention_pa_kernel(tc, x, freqs, wq, wk, wv, out_0, out_1, out_2):
                     op=MULT,
                 )
             rotated = results.tile([P, width], F32, name="rotated")
-            nc.vector.tensor_tensor(
+            nc.gpsimd.tensor_tensor(
                 out=rotated[:].rearrange("p (c e) -> p c e", e=2),
                 in0=by_cos[:].rearrange("p (c e) -> p c e", e=2),
                 in1=by_sin[:].rearrange("p e c -> p c e"),

@@ -29,7 +29,7 @@ KV_WIDTH = 2 * HEAD
 CHUNK = 512
 CHUNK_BLOCKS = CHUNK // P
 CHUNKS = (Q_WIDTH + 2 * KV_WIDTH) // CHUNK
-X_AHEAD = 2
+X_AHEAD = 3
 
 FLOPS = 2 * TOKENS * FEATURES * (Q_WIDTH + 2 * KV_WIDTH)
 
@@ -63,8 +63,7 @@ def tile_attention_pa_kernel(tc, x, freqs, wq, wk, wv, out_0, out_1, out_2):
         raw = ctx.enter_context(tc.tile_pool(name="raw", bufs=1))
         tables = ctx.enter_context(tc.tile_pool(name="tables", bufs=1))
         quantised = ctx.enter_context(tc.tile_pool(name="quantised", bufs=1))
-        x_stage = ctx.enter_context(tc.tile_pool(name="x_stage", bufs=3))
-        w_stage = ctx.enter_context(tc.tile_pool(name="w_stage", bufs=1))
+        stage = ctx.enter_context(tc.tile_pool(name="stage", bufs=5))
         work = ctx.enter_context(tc.tile_pool(name="work", bufs=6))
         results = ctx.enter_context(tc.tile_pool(name="results", bufs=6))
         turned = ctx.enter_context(tc.psum_pool(name="turned", bufs=4))
@@ -130,9 +129,10 @@ def tile_attention_pa_kernel(tc, x, freqs, wq, wk, wv, out_0, out_1, out_2):
         x_scales = [quantised.tile([P, PASSES * P], U8, name="x_scales%d" % t, align_bytes=64) for t in range(TOKEN_TILES)]
         w_codes = [quantised.tile([P, PASSES, CHUNK], U32, name="w_codes%d" % c, align_bytes=64) for c in range(CHUNKS)]
         w_scales = [quantised.tile([P, PASSES, CHUNK], U8, name="w_scales%d" % c, align_bytes=64) for c in range(CHUNKS)]
-        w_grouped = {}
 
-        def transpose_block(rows, grouped_words):
+        def transpose_block(rows):
+            grouped = stage.tile([P, PASSES * P * PACK], BF16, align_bytes=64)
+            grouped_words = grouped[:].bitcast(F32).rearrange("p (g r u) -> p g r u", g=PASSES, u=2)
             words = rows[:].bitcast(F32)
             for first_pass in range(0, PASSES, 2):
                 bank = turned.tile([P, 2, 2, P], F32)
@@ -144,30 +144,23 @@ def tile_attention_pa_kernel(tc, x, freqs, wq, wk, wv, out_0, out_1, out_2):
                     out=grouped_words[:, first_pass : first_pass + 2, :, :],
                     in_=bank[:].rearrange("p g u r -> p g r u"),
                 )
+            return grouped
 
         def prepare(block):
             kind, index = block
             if kind == "x":
-                grouped = x_stage.tile([P, PASSES * P * PACK], BF16, align_bytes=64)
-                transpose_block(
-                    x_raw[index], grouped[:].bitcast(F32).rearrange("p (g r u) -> p g r u", g=PASSES, u=2)
-                )
+                grouped = transpose_block(x_raw[index])
                 nc.vector.quantize_mx(
                     out=x_codes[index][:].bitcast(FP8X4), scales=x_scales[index][:], in_=grouped[:]
                 )
-                return
-            chunk, place = divmod(index, CHUNK_BLOCKS)
-            if place == 0:
-                w_grouped[chunk] = w_stage.tile([P, PASSES * CHUNK * PACK], BF16, name="w_grouped", align_bytes=64)
-            grouped = w_grouped[chunk]
-            grouped_words = grouped[:].bitcast(F32).rearrange("p (g r u) -> p g r u", g=PASSES, u=2)
-            transpose_block(w_raw[index], grouped_words[:, :, place * P : (place + 1) * P, :])
-            if place == CHUNK_BLOCKS - 1:
+            else:
+                chunk, place = divmod(index, CHUNK_BLOCKS)
+                grouped = transpose_block(w_raw[index])
                 for g in range(PASSES):
                     nc.vector.quantize_mx(
-                        out=w_codes[chunk][:, g, :].bitcast(FP8X4),
-                        scales=w_scales[chunk][:, g, :],
-                        in_=grouped[:, g * CHUNK * PACK : (g + 1) * CHUNK * PACK],
+                        out=w_codes[chunk][:, g, place * P : (place + 1) * P].bitcast(FP8X4),
+                        scales=w_scales[chunk][:, g, place * P : (place + 1) * P],
+                        in_=grouped[:, g * P * PACK : (g + 1) * P * PACK],
                     )
 
         def project(tile, chunk, first_row, width):

@@ -66,6 +66,7 @@ def tile_attention_pa_kernel(tc, x, freqs, wq, wk, wv, out_0, out_1, out_2):
         stage = ctx.enter_context(tc.tile_pool(name="stage", bufs=5))
         work = ctx.enter_context(tc.tile_pool(name="work", bufs=6))
         results = ctx.enter_context(tc.tile_pool(name="results", bufs=6))
+        v_results = ctx.enter_context(tc.tile_pool(name="v_results", bufs=TOKEN_TILES))
         turned = ctx.enter_context(tc.psum_pool(name="turned", bufs=4))
         sums = ctx.enter_context(tc.psum_pool(name="sums", bufs=4))
 
@@ -99,31 +100,25 @@ def tile_attention_pa_kernel(tc, x, freqs, wq, wk, wv, out_0, out_1, out_2):
         nc.scalar.activation(out=sin_quarter[:], in_=angles[:].rearrange("p t i -> p (t i)"), func=SIN, scale=0.25)
 
         square_half = tables.tile([P, n_angles], F32)
-        cos_twice = tables.tile([P, POSITION_TILES, HEAD], F32)
-        nc.vector.tensor_tensor(out=square_half[:], in0=sin_half[:], in1=sin_half[:], op=MULT)
-        nc.vector.tensor_scalar(
-            out=cos_twice[:].rearrange("p t (i e) -> p (t i) e", e=2),
-            in0=square_half[:].unsqueeze(2).to_broadcast([P, n_angles, 2]),
-            scalar1=-2.0,
-            scalar2=1.0,
-            op0=MULT,
-            op1=ADD,
-        )
         square_quarter = tables.tile([P, n_angles], F32)
         cos_half = tables.tile([P, n_angles], F32)
         half_sin = tables.tile([P, n_angles], F32)
-        signed_sin = tables.tile([P, POSITION_TILES, 2, PAIRS], F32)
+        nc.vector.tensor_tensor(out=square_half[:], in0=sin_half[:], in1=sin_half[:], op=MULT)
         nc.vector.tensor_tensor(out=square_quarter[:], in0=sin_quarter[:], in1=sin_quarter[:], op=MULT)
         nc.vector.tensor_scalar(
             out=cos_half[:], in0=square_quarter[:], scalar1=-2.0, scalar2=1.0, op0=MULT, op1=ADD
         )
         nc.vector.tensor_tensor(out=half_sin[:], in0=sin_half[:], in1=cos_half[:], op=MULT)
-        for e, factor in ((0, -2.0), (1, 2.0)):
-            nc.vector.tensor_scalar_mul(
-                out=signed_sin[:, :, e, :],
-                in0=half_sin[:].rearrange("p (t i) -> p t i", i=PAIRS),
-                scalar1=factor,
+        from_even = tables.tile([P, POSITION_TILES, PAIRS, 2], F32)
+        from_odd = tables.tile([P, POSITION_TILES, PAIRS, 2], F32)
+        even_factors = from_even[:].rearrange("p t i j -> p (t i) j")
+        odd_factors = from_odd[:].rearrange("p t i j -> p (t i) j")
+        for cos_place in (even_factors[:, :, 0], odd_factors[:, :, 1]):
+            nc.vector.tensor_scalar(
+                out=cos_place, in0=square_half[:], scalar1=-2.0, scalar2=1.0, op0=MULT, op1=ADD
             )
+        nc.vector.tensor_scalar_mul(out=even_factors[:, :, 1], in0=half_sin[:], scalar1=2.0)
+        nc.vector.tensor_scalar_mul(out=odd_factors[:, :, 0], in0=half_sin[:], scalar1=-2.0)
 
         x_codes = [quantised.tile([P, PASSES * P], U32, name="x_codes%d" % t, align_bytes=64) for t in range(TOKEN_TILES)]
         x_scales = [quantised.tile([P, PASSES * P], U8, name="x_scales%d" % t, align_bytes=64) for t in range(TOKEN_TILES)]
@@ -180,47 +175,38 @@ def tile_attention_pa_kernel(tc, x, freqs, wq, wk, wv, out_0, out_1, out_2):
         def rotate(total, tile, width):
             heads = width // HEAD
             t = tile % POSITION_TILES
-            by_cos = work.tile([P, width], F32, name="by_cos")
-            nc.vector.tensor_tensor(
-                out=by_cos[:].rearrange("p (h c) -> p h c", h=heads),
-                in0=total[:].rearrange("p (h c) -> p h c", h=heads),
-                in1=cos_twice[:, t, :].unsqueeze(1).to_broadcast([P, heads, HEAD]),
-                op=MULT,
-            )
-            by_sin = work.tile([P, 2, heads * PAIRS], F32, name="by_sin")
-            features = total[:].rearrange("p (h i e) -> p e h i", h=heads, e=2)
-            for e in range(2):
+            features = total[:].rearrange("p (h i e) -> p h i e", h=heads, e=2)
+            parts = []
+            for e, factors in ((0, from_even), (1, from_odd)):
+                part = work.tile([P, width], F32, name="part%d" % e)
                 nc.vector.tensor_tensor(
-                    out=by_sin[:, e, :].rearrange("p (h i) -> p h i", h=heads),
-                    in0=features[:, 1 - e, :, :],
-                    in1=signed_sin[:, t, e, :].unsqueeze(1).to_broadcast([P, heads, PAIRS]),
+                    out=part[:].rearrange("p (h i j) -> p h i j", h=heads, j=2),
+                    in0=features[:, :, :, e : e + 1].to_broadcast([P, heads, PAIRS, 2]),
+                    in1=factors[:, t, :, :].unsqueeze(1).to_broadcast([P, heads, PAIRS, 2]),
                     op=MULT,
                 )
+                parts.append(part)
             rotated = results.tile([P, width], F32, name="rotated")
-            nc.gpsimd.tensor_tensor(
-                out=rotated[:].rearrange("p (c e) -> p c e", e=2),
-                in0=by_cos[:].rearrange("p (c e) -> p c e", e=2),
-                in1=by_sin[:].rearrange("p e c -> p c e"),
-                op=ADD,
-            )
+            nc.gpsimd.tensor_tensor(out=rotated[:], in0=parts[0][:], in1=parts[1][:], op=ADD)
             return rotated
 
         for block in first_blocks:
             prepare(block)
-        for chunk in range(CHUNKS):
+        for chunk in range(Q_WIDTH // CHUNK):
             for tile in range(TOKEN_TILES):
-                tokens = slice(tile * P, (tile + 1) * P)
-                if chunk * CHUNK < Q_WIDTH:
-                    total = project(tile, chunk, 0, CHUNK)
-                    rotated = rotate(total, tile, CHUNK)
-                    nc.sync.dma_start(out=q_rows[tokens, chunk * CHUNK : (chunk + 1) * CHUNK], in_=rotated[:])
-                else:
-                    k_total = project(tile, chunk, 0, KV_WIDTH)
-                    v_total = project(tile, chunk, KV_WIDTH, KV_WIDTH)
-                    k_rotated = rotate(k_total, tile, KV_WIDTH)
-                    nc.sync.dma_start(out=k_rows[tokens, :], in_=k_rotated[:])
-                    v_copy = results.tile([P, KV_WIDTH], F32)
-                    nc.scalar.copy(out=v_copy[:], in_=v_total[:])
-                    nc.sync.dma_start(out=v_rows[tokens, :], in_=v_copy[:])
+                total = project(tile, chunk, 0, CHUNK)
+                rotated = rotate(total, tile, CHUNK)
+                nc.sync.dma_start(
+                    out=q_rows[tile * P : (tile + 1) * P, chunk * CHUNK : (chunk + 1) * CHUNK], in_=rotated[:]
+                )
                 for block in blocks_after(chunk, tile):
                     prepare(block)
+        for tile in range(TOKEN_TILES):
+            total = project(tile, CHUNKS - 1, 0, KV_WIDTH)
+            rotated = rotate(total, tile, KV_WIDTH)
+            nc.sync.dma_start(out=k_rows[tile * P : (tile + 1) * P, :], in_=rotated[:])
+        for tile in range(TOKEN_TILES):
+            total = project(tile, CHUNKS - 1, KV_WIDTH, KV_WIDTH)
+            v_copy = v_results.tile([P, KV_WIDTH], F32)
+            nc.scalar.copy(out=v_copy[:], in_=total[:])
+            nc.sync.dma_start(out=v_rows[tile * P : (tile + 1) * P, :], in_=v_copy[:])

@@ -64,11 +64,11 @@ def tile_attention_pa_kernel(tc, x, freqs, wq, wk, wv, out_0, out_1, out_2):
         tables = ctx.enter_context(tc.tile_pool(name="tables", bufs=1))
         quantised = ctx.enter_context(tc.tile_pool(name="quantised", bufs=1))
         stage = ctx.enter_context(tc.tile_pool(name="stage", bufs=5))
-        work = ctx.enter_context(tc.tile_pool(name="work", bufs=6))
+        q_parts = ctx.enter_context(tc.tile_pool(name="q_parts", bufs=6))
+        k_parts = ctx.enter_context(tc.tile_pool(name="k_parts", bufs=TOKEN_TILES))
         results = ctx.enter_context(tc.tile_pool(name="results", bufs=6))
-        v_results = ctx.enter_context(tc.tile_pool(name="v_results", bufs=TOKEN_TILES))
-        turned = ctx.enter_context(tc.psum_pool(name="turned", bufs=4))
-        sums = ctx.enter_context(tc.psum_pool(name="sums", bufs=4))
+        kv_results = ctx.enter_context(tc.tile_pool(name="kv_results", bufs=TOKEN_TILES))
+        banks = ctx.enter_context(tc.psum_pool(name="banks", bufs=4))
 
         x_raw = [raw.tile([P, FEATURES], BF16, name="x_raw%d" % t) for t in range(TOKEN_TILES)]
         w_raw = [raw.tile([P, FEATURES], BF16, name="w_raw%d" % b) for b in range(CHUNKS * CHUNK_BLOCKS)]
@@ -130,7 +130,7 @@ def tile_attention_pa_kernel(tc, x, freqs, wq, wk, wv, out_0, out_1, out_2):
             grouped_words = grouped[:].bitcast(F32).rearrange("p (g r u) -> p g r u", g=PASSES, u=2)
             words = rows[:].bitcast(F32)
             for first_pass in range(0, PASSES, 2):
-                bank = turned.tile([P, 2, 2, P], F32)
+                bank = banks.tile([P, 2, 2, P], F32, tag="turned")
                 for g in range(2):
                     for u in range(2):
                         first_word = (2 * (first_pass + g) + u) * P
@@ -158,8 +158,8 @@ def tile_attention_pa_kernel(tc, x, freqs, wq, wk, wv, out_0, out_1, out_2):
                         in_=grouped[:, g * P * PACK : (g + 1) * P * PACK],
                     )
 
-        def project(tile, chunk, first_row, width):
-            total = sums.tile([P, width], F32, name="total")
+        def project(tile, chunk, first_row, width, bank_tag):
+            total = banks.tile([P, width], F32, tag=bank_tag)
             for g in range(PASSES):
                 nc.tensor.matmul_mx(
                     out=total[:],
@@ -172,13 +172,13 @@ def tile_attention_pa_kernel(tc, x, freqs, wq, wk, wv, out_0, out_1, out_2):
                 )
             return total
 
-        def rotate(total, tile, width):
+        def rotation_parts(total, tile, width, pool):
             heads = width // HEAD
             t = tile % POSITION_TILES
             features = total[:].rearrange("p (h i e) -> p h i e", h=heads, e=2)
             parts = []
             for e, factors in ((0, from_even), (1, from_odd)):
-                part = work.tile([P, width], F32, name="part%d" % e)
+                part = pool.tile([P, width], F32, name="part%d" % e)
                 nc.vector.tensor_tensor(
                     out=part[:].rearrange("p (h i j) -> p h i j", h=heads, j=2),
                     in0=features[:, :, :, e : e + 1].to_broadcast([P, heads, PAIRS, 2]),
@@ -186,27 +186,30 @@ def tile_attention_pa_kernel(tc, x, freqs, wq, wk, wv, out_0, out_1, out_2):
                     op=MULT,
                 )
                 parts.append(part)
-            rotated = results.tile([P, width], F32, name="rotated")
-            nc.gpsimd.tensor_tensor(out=rotated[:], in0=parts[0][:], in1=parts[1][:], op=ADD)
-            return rotated
+            return parts
 
         for block in first_blocks:
             prepare(block)
         for chunk in range(Q_WIDTH // CHUNK):
             for tile in range(TOKEN_TILES):
-                total = project(tile, chunk, 0, CHUNK)
-                rotated = rotate(total, tile, CHUNK)
+                total = project(tile, chunk, 0, CHUNK, "sums")
+                parts = rotation_parts(total, tile, CHUNK, q_parts)
+                rotated = results.tile([P, CHUNK], F32, name="q_rotated")
+                nc.gpsimd.tensor_tensor(out=rotated[:], in0=parts[0][:], in1=parts[1][:], op=ADD)
                 nc.sync.dma_start(
                     out=q_rows[tile * P : (tile + 1) * P, chunk * CHUNK : (chunk + 1) * CHUNK], in_=rotated[:]
                 )
                 for block in blocks_after(chunk, tile):
                     prepare(block)
+        k_halves = []
         for tile in range(TOKEN_TILES):
-            total = project(tile, CHUNKS - 1, 0, KV_WIDTH)
-            rotated = rotate(total, tile, KV_WIDTH)
+            total = project(tile, CHUNKS - 1, 0, KV_WIDTH, ("sums", "turned")[tile % 2])
+            k_halves.append(rotation_parts(total, tile, KV_WIDTH, k_parts))
+        for tile in range(TOKEN_TILES):
+            total = project(tile, CHUNKS - 1, KV_WIDTH, KV_WIDTH, ("sums", "turned")[tile % 2])
+            rotated = kv_results.tile([P, KV_WIDTH], F32, name="k_rotated")
+            nc.vector.tensor_tensor(out=rotated[:], in0=k_halves[tile][0][:], in1=k_halves[tile][1][:], op=ADD)
             nc.sync.dma_start(out=k_rows[tile * P : (tile + 1) * P, :], in_=rotated[:])
-        for tile in range(TOKEN_TILES):
-            total = project(tile, CHUNKS - 1, KV_WIDTH, KV_WIDTH)
-            v_copy = v_results.tile([P, KV_WIDTH], F32)
+            v_copy = kv_results.tile([P, KV_WIDTH], F32)
             nc.scalar.copy(out=v_copy[:], in_=total[:])
             nc.sync.dma_start(out=v_rows[tile * P : (tile + 1) * P, :], in_=v_copy[:])

@@ -17,45 +17,45 @@ PACK = 4
 K_PASS = P * PACK
 FEATURES = 2048
 PASSES = FEATURES // K_PASS
-WORDS = FEATURES // 2
 TOKENS = 2 * 16 * 32
-TOKEN_TILES = TOKENS // P
-POSITIONS = 16 * 32
-POSITION_TILES = POSITIONS // P
+POSITION_TILES = 16 * 32 // P
 HEAD = 128
 PAIRS = HEAD // 2
-Q_WIDTH = 8 * HEAD
-KV_WIDTH = 2 * HEAD
-CHUNK = 512
-CHUNK_BLOCKS = CHUNK // P
-CHUNKS = (Q_WIDTH + 2 * KV_WIDTH) // CHUNK
-X_AHEAD = 3
+W_PAIR = 2 * P
+W_PAIRS = 6
+X_PAIRS = POSITION_TILES
 
-FLOPS = 2 * TOKENS * FEATURES * (Q_WIDTH + 2 * KV_WIDTH)
+FLOPS = 2 * TOKENS * FEATURES * W_PAIRS * W_PAIR
+
+GROUPS = (("w", 0), ("x", 0), ("w", 1), ("x", 1), ("w", 2), ("x", 2), ("w", 3), ("x", 3), ("w", 4), ("w", 5))
+LAST = len(GROUPS) - 1
 
 
-def blocks_after(chunk, tile):
-    blocks = []
-    if chunk == 0 and tile + X_AHEAD < TOKEN_TILES:
-        blocks.append(("x", tile + X_AHEAD))
-    if chunk + 1 < CHUNKS and tile < CHUNK_BLOCKS:
-        blocks.append(("w", (chunk + 1) * CHUNK_BLOCKS + tile))
-    return blocks
+def units_of(step):
+    kind, index = GROUPS[step]
+    seen = [i for k, i in GROUPS[:step] if k != kind]
+    return [(i, index) if kind == "x" else (index, i) for i in seen]
 
 
 def tile_attention_pa_kernel(tc, x, freqs, wq, wk, wv, out_0, out_1, out_2):
     nc = tc.nc
     x_rows = x.rearrange("b s k d -> (b s k) d")
     angle_rows = freqs.rearrange("s k i -> (s k) i")
-    q_rows = out_0.rearrange("b s k h d -> (b s k) (h d)")
-    k_rows = out_1.rearrange("b s k h d -> (b s k) (h d)")
-    v_rows = out_2.rearrange("b s k h d -> (b s k) (h d)")
+    q_view = out_0.rearrange("b s k h d -> b (s k) (h d)")
+    k_view = out_1.rearrange("b s k h d -> b (s k) (h d)")
+    v_view = out_2.rearrange("b s k h d -> b (s k) (h d)")
 
     w_block_rows = (
-        [wq[r : r + P, :] for r in range(0, Q_WIDTH, P)]
-        + [wk[r : r + P, :] for r in range(0, KV_WIDTH, P)]
-        + [wv[r : r + P, :] for r in range(0, KV_WIDTH, P)]
+        [wk[r : r + P, :] for r in range(0, W_PAIR, P)]
+        + [wq[r : r + P, :] for r in range(0, 4 * W_PAIR, P)]
+        + [wv[r : r + P, :] for r in range(0, W_PAIR, P)]
     )
+
+    def block_rows(group):
+        kind, index = group
+        if kind == "w":
+            return w_block_rows[2 * index : 2 * index + 2]
+        return [x_rows[t * P : (t + 1) * P, :] for t in (index, index + X_PAIRS)]
 
     with ExitStack() as ctx:
         ctx.enter_context(tc.manual_schedule())
@@ -63,30 +63,19 @@ def tile_attention_pa_kernel(tc, x, freqs, wq, wk, wv, out_0, out_1, out_2):
         raw = ctx.enter_context(tc.tile_pool(name="raw", bufs=1))
         tables = ctx.enter_context(tc.tile_pool(name="tables", bufs=1))
         quantised = ctx.enter_context(tc.tile_pool(name="quantised", bufs=1))
-        stage = ctx.enter_context(tc.tile_pool(name="stage", bufs=5))
-        q_parts = ctx.enter_context(tc.tile_pool(name="q_parts", bufs=6))
-        k_parts = ctx.enter_context(tc.tile_pool(name="k_parts", bufs=TOKEN_TILES))
-        results = ctx.enter_context(tc.tile_pool(name="results", bufs=6))
-        kv_results = ctx.enter_context(tc.tile_pool(name="kv_results", bufs=TOKEN_TILES))
+        stage = ctx.enter_context(tc.tile_pool(name="stage", bufs=3))
+        parts_pool = ctx.enter_context(tc.tile_pool(name="parts", bufs=6))
+        results = ctx.enter_context(tc.tile_pool(name="results", bufs=8))
         banks = ctx.enter_context(tc.psum_pool(name="banks", bufs=4))
 
-        x_raw = [raw.tile([P, FEATURES], BF16, name="x_raw%d" % t) for t in range(TOKEN_TILES)]
-        w_raw = [raw.tile([P, FEATURES], BF16, name="w_raw%d" % b) for b in range(CHUNKS * CHUNK_BLOCKS)]
-
-        def load(block):
-            kind, index = block
-            if kind == "x":
-                nc.sync.dma_start(out=x_raw[index][:], in_=x_rows[index * P : (index + 1) * P, :])
-            else:
-                nc.sync.dma_start(out=w_raw[index][:], in_=w_block_rows[index])
-
-        first_blocks = [("w", b) for b in range(CHUNK_BLOCKS)] + [("x", t) for t in range(X_AHEAD)]
-        for block in first_blocks:
-            load(block)
-        for chunk in range(CHUNKS):
-            for tile in range(TOKEN_TILES):
-                for block in blocks_after(chunk, tile):
-                    load(block)
+        raw_tiles = []
+        for s, group in enumerate(GROUPS):
+            pair = []
+            for b, rows in enumerate(block_rows(group)):
+                raw_tile = raw.tile([P, FEATURES], BF16, name="raw%d_%d" % (s, b))
+                nc.sync.dma_start(out=raw_tile[:], in_=rows)
+                pair.append(raw_tile)
+            raw_tiles.append(pair)
 
         angles = tables.tile([P, POSITION_TILES, PAIRS], BF16)
         nc.scalar.dma_start(out=angles[:], in_=angle_rows.rearrange("(t p) i -> p t i", p=P))
@@ -120,96 +109,107 @@ def tile_attention_pa_kernel(tc, x, freqs, wq, wk, wv, out_0, out_1, out_2):
         nc.vector.tensor_scalar_mul(out=even_factors[:, :, 1], in0=half_sin[:], scalar1=2.0)
         nc.vector.tensor_scalar_mul(out=odd_factors[:, :, 0], in0=half_sin[:], scalar1=-2.0)
 
-        x_codes = [quantised.tile([P, PASSES * P], U32, name="x_codes%d" % t, align_bytes=64) for t in range(TOKEN_TILES)]
-        x_scales = [quantised.tile([P, PASSES * P], U8, name="x_scales%d" % t, align_bytes=64) for t in range(TOKEN_TILES)]
-        w_codes = [quantised.tile([P, PASSES, CHUNK], U32, name="w_codes%d" % c, align_bytes=64) for c in range(CHUNKS)]
-        w_scales = [quantised.tile([P, PASSES, CHUNK], U8, name="w_scales%d" % c, align_bytes=64) for c in range(CHUNKS)]
+        x_codes = [quantised.tile([P, 2, PASSES, P], U32, name="x_codes%d" % j, align_bytes=64) for j in range(X_PAIRS)]
+        x_scales = [quantised.tile([P, 2, PASSES, P], U8, name="x_scales%d" % j, align_bytes=64) for j in range(X_PAIRS)]
+        w_codes = [quantised.tile([P, PASSES, W_PAIR], U32, name="w_codes%d" % i, align_bytes=64) for i in range(W_PAIRS)]
+        w_scales = [quantised.tile([P, PASSES, W_PAIR], U8, name="w_scales%d" % i, align_bytes=64) for i in range(W_PAIRS)]
 
-        def transpose_block(rows):
-            grouped = stage.tile([P, PASSES * P * PACK], BF16, align_bytes=64)
-            grouped_words = grouped[:].bitcast(F32).rearrange("p (g r u) -> p g r u", g=PASSES, u=2)
-            words = rows[:].bitcast(F32)
-            for first_pass in range(0, PASSES, 2):
-                bank = banks.tile([P, 2, 2, P], F32, tag="turned")
-                for g in range(2):
-                    for u in range(2):
-                        first_word = (2 * (first_pass + g) + u) * P
-                        nc.tensor.transpose(bank[:, g, u, :], words[:, first_word : first_word + P], identity[:])
-                nc.scalar.copy(
-                    out=grouped_words[:, first_pass : first_pass + 2, :, :],
-                    in_=bank[:].rearrange("p g u r -> p g r u"),
-                )
+        def transpose_group(step):
+            kind, index = GROUPS[step]
+            grouped = stage.tile([P, 2 * PASSES * P * PACK], BF16, align_bytes=64)
+            words_out = grouped[:].bitcast(F32)
+            for b in range(2):
+                words = raw_tiles[step][b][:].bitcast(F32)
+                for first_pass in range(0, PASSES, 2):
+                    bank = banks.tile([P, 2, 2, P], F32, tag="turned")
+                    for g in range(2):
+                        for u in range(2):
+                            first_word = (2 * (first_pass + g) + u) * P
+                            nc.tensor.transpose(bank[:, g, u, :], words[:, first_word : first_word + P], identity[:])
+                    if kind == "x":
+                        place = words_out.rearrange("p (b g r u) -> p b g r u", b=2, g=PASSES, u=2)[:, b]
+                    else:
+                        place = words_out.rearrange("p (g b r u) -> p b g r u", b=2, g=PASSES, u=2)[:, b]
+                    nc.scalar.copy(
+                        out=place[:, first_pass : first_pass + 2, :, :],
+                        in_=bank[:].rearrange("p g u r -> p g r u"),
+                    )
             return grouped
 
-        def prepare(block):
-            kind, index = block
-            if kind == "x":
-                grouped = transpose_block(x_raw[index])
-                nc.vector.quantize_mx(
-                    out=x_codes[index][:].bitcast(FP8X4), scales=x_scales[index][:], in_=grouped[:]
-                )
-            else:
-                chunk, place = divmod(index, CHUNK_BLOCKS)
-                grouped = transpose_block(w_raw[index])
-                for g in range(PASSES):
-                    nc.vector.quantize_mx(
-                        out=w_codes[chunk][:, g, place * P : (place + 1) * P].bitcast(FP8X4),
-                        scales=w_scales[chunk][:, g, place * P : (place + 1) * P],
-                        in_=grouped[:, g * P * PACK : (g + 1) * P * PACK],
-                    )
+        def quantise_group(step, grouped):
+            kind, index = GROUPS[step]
+            for half in range(2):
+                values = grouped[:, half * FEATURES : (half + 1) * FEATURES]
+                if kind == "x":
+                    codes = x_codes[index][:, half].rearrange("p g r -> p (g r)")
+                    scales = x_scales[index][:, half].rearrange("p g r -> p (g r)")
+                else:
+                    codes = w_codes[index][:, 2 * half : 2 * half + 2].rearrange("p g r -> p (g r)")
+                    scales = w_scales[index][:, 2 * half : 2 * half + 2].rearrange("p g r -> p (g r)")
+                nc.vector.quantize_mx(out=codes.bitcast(FP8X4), scales=scales, in_=values)
 
-        def project(tile, chunk, first_row, width, bank_tag):
-            total = banks.tile([P, width], F32, tag=bank_tag)
-            for g in range(PASSES):
-                nc.tensor.matmul_mx(
-                    out=total[:],
-                    lhsT=x_codes[tile][:, g * P : (g + 1) * P].bitcast(FP8X4),
-                    lhsT_scale=x_scales[tile][:, g * P : (g + 1) * P],
-                    rhs=w_codes[chunk][:, g, first_row : first_row + width].bitcast(FP8X4),
-                    rhs_scale=w_scales[chunk][:, g, first_row : first_row + width],
-                    start=(g == 0),
-                    stop=(g == PASSES - 1),
-                )
+        def project(unit, tag):
+            w_index, x_index = unit
+            total = banks.tile([P, 2, W_PAIR], F32, tag=tag)
+            for b in range(2):
+                for g in range(PASSES):
+                    nc.tensor.matmul_mx(
+                        out=total[:, b, :],
+                        lhsT=x_codes[x_index][:, b, g, :].bitcast(FP8X4),
+                        lhsT_scale=x_scales[x_index][:, b, g, :],
+                        rhs=w_codes[w_index][:, g, :].bitcast(FP8X4),
+                        rhs_scale=w_scales[w_index][:, g, :],
+                        start=(g == 0),
+                        stop=(g == PASSES - 1),
+                    )
             return total
 
-        def rotation_parts(total, tile, width, pool):
-            heads = width // HEAD
-            t = tile % POSITION_TILES
-            features = total[:].rearrange("p (h i e) -> p h i e", h=heads, e=2)
-            parts = []
-            for e, factors in ((0, from_even), (1, from_odd)):
-                part = pool.tile([P, width], F32, name="part%d" % e)
-                nc.vector.tensor_tensor(
-                    out=part[:].rearrange("p (h i j) -> p h i j", h=heads, j=2),
-                    in0=features[:, :, :, e : e + 1].to_broadcast([P, heads, PAIRS, 2]),
-                    in1=factors[:, t, :, :].unsqueeze(1).to_broadcast([P, heads, PAIRS, 2]),
-                    op=MULT,
-                )
-                parts.append(part)
-            return parts
+        def store(unit, rows):
+            w_index, x_index = unit
+            positions = slice(x_index * P, (x_index + 1) * P)
+            if w_index == 0:
+                place = k_view[:, positions, :]
+            elif w_index == W_PAIRS - 1:
+                place = v_view[:, positions, :]
+            else:
+                place = q_view[:, positions, (w_index - 1) * W_PAIR : w_index * W_PAIR]
+            nc.sync.dma_start(out=place.rearrange("b p n -> p b n"), in_=rows[:].rearrange("p (b n) -> p b n", b=2))
 
-        for block in first_blocks:
-            prepare(block)
-        for chunk in range(Q_WIDTH // CHUNK):
-            for tile in range(TOKEN_TILES):
-                total = project(tile, chunk, 0, CHUNK, "sums")
-                parts = rotation_parts(total, tile, CHUNK, q_parts)
-                rotated = results.tile([P, CHUNK], F32, name="q_rotated")
-                nc.gpsimd.tensor_tensor(out=rotated[:], in0=parts[0][:], in1=parts[1][:], op=ADD)
-                nc.sync.dma_start(
-                    out=q_rows[tile * P : (tile + 1) * P, chunk * CHUNK : (chunk + 1) * CHUNK], in_=rotated[:]
-                )
-                for block in blocks_after(chunk, tile):
-                    prepare(block)
-        k_halves = []
-        for tile in range(TOKEN_TILES):
-            total = project(tile, CHUNKS - 1, 0, KV_WIDTH, ("sums", "turned")[tile % 2])
-            k_halves.append(rotation_parts(total, tile, KV_WIDTH, k_parts))
-        for tile in range(TOKEN_TILES):
-            total = project(tile, CHUNKS - 1, KV_WIDTH, KV_WIDTH, ("sums", "turned")[tile % 2])
-            rotated = kv_results.tile([P, KV_WIDTH], F32, name="k_rotated")
-            nc.vector.tensor_tensor(out=rotated[:], in0=k_halves[tile][0][:], in1=k_halves[tile][1][:], op=ADD)
-            nc.sync.dma_start(out=k_rows[tile * P : (tile + 1) * P, :], in_=rotated[:])
-            v_copy = kv_results.tile([P, KV_WIDTH], F32)
-            nc.scalar.copy(out=v_copy[:], in_=total[:])
-            nc.sync.dma_start(out=v_rows[tile * P : (tile + 1) * P, :], in_=v_copy[:])
+        def finish(unit, total):
+            w_index, x_index = unit
+            flat = total[:].rearrange("p b n -> p (b n)")
+            rows = results.tile([P, 2 * W_PAIR], F32, name="rows")
+            if w_index == W_PAIRS - 1:
+                nc.scalar.copy(out=rows[:], in_=flat)
+            else:
+                heads = 2 * W_PAIR // HEAD
+                features = flat.rearrange("p (h i e) -> p h i e", h=heads, e=2)
+                parts = []
+                for e, factors in ((0, from_even), (1, from_odd)):
+                    part = parts_pool.tile([P, 2 * W_PAIR], F32, name="part%d" % e)
+                    nc.vector.tensor_tensor(
+                        out=part[:].rearrange("p (h i j) -> p h i j", h=heads, j=2),
+                        in0=features[:, :, :, e : e + 1].to_broadcast([P, heads, PAIRS, 2]),
+                        in1=factors[:, x_index, :, :].unsqueeze(1).to_broadcast([P, heads, PAIRS, 2]),
+                        op=MULT,
+                    )
+                    parts.append(part)
+                nc.gpsimd.tensor_tensor(out=rows[:], in0=parts[0][:], in1=parts[1][:], op=ADD)
+            store(unit, rows)
+
+        for step in range(2):
+            quantise_group(step, transpose_group(step))
+        for step in range(1, LAST - 1):
+            grouped = transpose_group(step + 1)
+            quantise_group(step + 1, grouped)
+            for unit in units_of(step):
+                finish(unit, project(unit, "sums"))
+        quantise_group(LAST, transpose_group(LAST))
+        q_units = units_of(LAST - 1)
+        v_units = units_of(LAST)
+        order = [q_units[0]]
+        for i in range(1, X_PAIRS):
+            order += [q_units[i], v_units[i - 1]]
+        order.append(v_units[X_PAIRS - 1])
+        for i, unit in enumerate(order):
+            finish(unit, project(unit, ("sums", "turned")[i % 2]))

@@ -65,7 +65,7 @@ def tile_attention_pa_kernel(tc, x, freqs, wq, wk, wv, out_0, out_1, out_2):
         quantised = ctx.enter_context(tc.tile_pool(name="quantised", bufs=1))
         stage = ctx.enter_context(tc.tile_pool(name="stage", bufs=3))
         parts_pool = ctx.enter_context(tc.tile_pool(name="parts", bufs=6))
-        results = ctx.enter_context(tc.tile_pool(name="results", bufs=8))
+        results = ctx.enter_context(tc.tile_pool(name="results", bufs=12))
         banks = ctx.enter_context(tc.psum_pool(name="banks", bufs=4))
 
         raw_tiles = []
@@ -109,10 +109,10 @@ def tile_attention_pa_kernel(tc, x, freqs, wq, wk, wv, out_0, out_1, out_2):
         nc.vector.tensor_scalar_mul(out=even_factors[:, :, 1], in0=half_sin[:], scalar1=2.0)
         nc.vector.tensor_scalar_mul(out=odd_factors[:, :, 0], in0=half_sin[:], scalar1=-2.0)
 
-        x_codes = [quantised.tile([P, 2, PASSES, P], U32, name="x_codes%d" % j, align_bytes=64) for j in range(X_PAIRS)]
-        x_scales = [quantised.tile([P, 2, PASSES, P], U8, name="x_scales%d" % j, align_bytes=64) for j in range(X_PAIRS)]
-        w_codes = [quantised.tile([P, PASSES, W_PAIR], U32, name="w_codes%d" % i, align_bytes=64) for i in range(W_PAIRS)]
-        w_scales = [quantised.tile([P, PASSES, W_PAIR], U8, name="w_scales%d" % i, align_bytes=64) for i in range(W_PAIRS)]
+        x_codes = [quantised.tile([P, 2, PASSES, P], U32, name="x_codes%d" % j, align_bytes=256) for j in range(X_PAIRS)]
+        x_scales = [quantised.tile([P, 2, PASSES, P], U8, name="x_scales%d" % j, align_bytes=256) for j in range(X_PAIRS)]
+        w_codes = [quantised.tile([P, PASSES, W_PAIR], U32, name="w_codes%d" % i, align_bytes=256) for i in range(W_PAIRS)]
+        w_scales = [quantised.tile([P, PASSES, W_PAIR], U8, name="w_scales%d" % i, align_bytes=256) for i in range(W_PAIRS)]
 
         def transpose_group(step):
             kind, index = GROUPS[step]
@@ -149,22 +149,12 @@ def tile_attention_pa_kernel(tc, x, freqs, wq, wk, wv, out_0, out_1, out_2):
                 nc.vector.quantize_mx(out=codes.bitcast(FP8X4), scales=scales, in_=values)
 
         def project(unit, tag):
-            w_index, x_index = unit
             total = banks.tile([P, 2, W_PAIR], F32, tag=tag)
             for b in range(2):
-                for g in range(PASSES):
-                    nc.tensor.matmul_mx(
-                        out=total[:, b, :],
-                        lhsT=x_codes[x_index][:, b, g, :].bitcast(FP8X4),
-                        lhsT_scale=x_scales[x_index][:, b, g, :],
-                        rhs=w_codes[w_index][:, g, :].bitcast(FP8X4),
-                        rhs_scale=w_scales[w_index][:, g, :],
-                        start=(g == 0),
-                        stop=(g == PASSES - 1),
-                    )
+                multiply(total[:, b, :], unit, b)
             return total
 
-        def store(unit, rows):
+        def place_of(unit):
             w_index, x_index = unit
             positions = slice(x_index * P, (x_index + 1) * P)
             if w_index == 0:
@@ -173,7 +163,7 @@ def tile_attention_pa_kernel(tc, x, freqs, wq, wk, wv, out_0, out_1, out_2):
                 place = v_view[:, positions, :]
             else:
                 place = q_view[:, positions, (w_index - 1) * W_PAIR : w_index * W_PAIR]
-            nc.sync.dma_start(out=place.rearrange("b p n -> p b n"), in_=rows[:].rearrange("p (b n) -> p b n", b=2))
+            return place.rearrange("b p n -> p b n")
 
         def finish(unit, total):
             w_index, x_index = unit
@@ -195,7 +185,28 @@ def tile_attention_pa_kernel(tc, x, freqs, wq, wk, wv, out_0, out_1, out_2):
                     )
                     parts.append(part)
                 nc.gpsimd.tensor_tensor(out=rows[:], in0=parts[0][:], in1=parts[1][:], op=ADD)
-            store(unit, rows)
+            nc.sync.dma_start(out=place_of(unit), in_=rows[:].rearrange("p (b n) -> p b n", b=2))
+
+        def multiply(out, unit, b):
+            w_index, x_index = unit
+            for g in range(PASSES):
+                nc.tensor.matmul_mx(
+                    out=out,
+                    lhsT=x_codes[x_index][:, b, g, :].bitcast(FP8X4),
+                    lhsT_scale=x_scales[x_index][:, b, g, :],
+                    rhs=w_codes[w_index][:, g, :].bitcast(FP8X4),
+                    rhs_scale=w_scales[w_index][:, g, :],
+                    start=(g == 0),
+                    stop=(g == PASSES - 1),
+                )
+
+        def last_v_unit(unit):
+            for b in range(2):
+                total = banks.tile([P, W_PAIR], F32, tag=("sums", "turned")[b], name="half_total")
+                multiply(total[:], unit, b)
+                rows = results.tile([P, W_PAIR], F32, name="half_rows")
+                nc.scalar.copy(out=rows[:], in_=total[:])
+                nc.sync.dma_start(out=place_of(unit)[:, b, :], in_=rows[:])
 
         for step in range(2):
             quantise_group(step, transpose_group(step))
@@ -207,9 +218,7 @@ def tile_attention_pa_kernel(tc, x, freqs, wq, wk, wv, out_0, out_1, out_2):
         quantise_group(LAST, transpose_group(LAST))
         q_units = units_of(LAST - 1)
         v_units = units_of(LAST)
-        order = [q_units[0]]
-        for i in range(1, X_PAIRS):
-            order += [q_units[i], v_units[i - 1]]
-        order.append(v_units[X_PAIRS - 1])
+        order = q_units[:2] + v_units[:1] + q_units[2:] + v_units[1:-1]
         for i, unit in enumerate(order):
             finish(unit, project(unit, ("sums", "turned")[i % 2]))
+        last_v_unit(v_units[-1])

@@ -165,7 +165,7 @@ def tile_attention_pa_kernel(tc, x, freqs, wq, wk, wv, out_0, out_1, out_2):
                 place = q_view[:, positions, (w_index - 1) * W_PAIR : w_index * W_PAIR]
             return place.rearrange("b p n -> p b n")
 
-        def finish(unit, total):
+        def finish(unit, total, adder):
             w_index, x_index = unit
             flat = total[:].rearrange("p b n -> p (b n)")
             rows = results.tile([P, 2 * W_PAIR], F32, name="rows")
@@ -184,7 +184,7 @@ def tile_attention_pa_kernel(tc, x, freqs, wq, wk, wv, out_0, out_1, out_2):
                         op=MULT,
                     )
                     parts.append(part)
-                nc.gpsimd.tensor_tensor(out=rows[:], in0=parts[0][:], in1=parts[1][:], op=ADD)
+                adder.tensor_tensor(out=rows[:], in0=parts[0][:], in1=parts[1][:], op=ADD)
             nc.sync.dma_start(out=place_of(unit), in_=rows[:].rearrange("p (b n) -> p b n", b=2))
 
         def multiply(out, unit, b):
@@ -211,14 +211,19 @@ def tile_attention_pa_kernel(tc, x, freqs, wq, wk, wv, out_0, out_1, out_2):
         for step in range(2):
             quantise_group(step, transpose_group(step))
         for step in range(1, LAST - 1):
+            units = units_of(step)
             grouped = transpose_group(step + 1)
+            early = units[:1] if len(units) > 1 else []
+            for unit in early:
+                finish(unit, project(unit, "sums"), nc.gpsimd)
             quantise_group(step + 1, grouped)
-            for unit in units_of(step):
-                finish(unit, project(unit, "sums"))
+            for unit in units[len(early) :]:
+                finish(unit, project(unit, "sums"), nc.gpsimd if early else nc.vector)
         quantise_group(LAST, transpose_group(LAST))
         q_units = units_of(LAST - 1)
         v_units = units_of(LAST)
         order = q_units[:2] + v_units[:1] + q_units[2:] + v_units[1:-1]
         for i, unit in enumerate(order):
-            finish(unit, project(unit, ("sums", "turned")[i % 2]))
+            adder = nc.vector if unit == q_units[-1] else nc.gpsimd
+            finish(unit, project(unit, ("sums", "turned")[i % 2]), adder)
         last_v_unit(v_units[-1])

@@ -65,17 +65,20 @@ def tile_attention_pa_kernel(tc, x, freqs, wq, wk, wv, out_0, out_1, out_2):
         quantised = ctx.enter_context(tc.tile_pool(name="quantised", bufs=1))
         stage = ctx.enter_context(tc.tile_pool(name="stage", bufs=3))
         parts_pool = ctx.enter_context(tc.tile_pool(name="parts", bufs=6))
-        results = ctx.enter_context(tc.tile_pool(name="results", bufs=12))
+        results = ctx.enter_context(tc.tile_pool(name="results", bufs=10))
         banks = ctx.enter_context(tc.psum_pool(name="banks", bufs=4))
 
-        raw_tiles = []
-        for s, group in enumerate(GROUPS):
-            pair = []
-            for b, rows in enumerate(block_rows(group)):
-                raw_tile = raw.tile([P, FEATURES], BF16, name="raw%d_%d" % (s, b))
-                nc.sync.dma_start(out=raw_tile[:], in_=rows)
-                pair.append(raw_tile)
-            raw_tiles.append(pair)
+        raw_tiles = [
+            [raw.tile([P, FEATURES], BF16, name="raw%d_%d" % (s, b)) for b in range(2)] for s in range(len(GROUPS))
+        ]
+        for half in range(2):
+            columns = slice(half * FEATURES // 2, (half + 1) * FEATURES // 2)
+            for step in range(2):
+                for b, rows in enumerate(block_rows(GROUPS[step])):
+                    nc.sync.dma_start(out=raw_tiles[step][b][:, columns], in_=rows[:, columns])
+        for step in range(2, len(GROUPS)):
+            for b, rows in enumerate(block_rows(GROUPS[step])):
+                nc.sync.dma_start(out=raw_tiles[step][b][:], in_=rows)
 
         angles = tables.tile([P, POSITION_TILES, PAIRS], BF16)
         nc.scalar.dma_start(out=angles[:], in_=angle_rows.rearrange("(t p) i -> p t i", p=P))
@@ -88,51 +91,72 @@ def tile_attention_pa_kernel(tc, x, freqs, wq, wk, wv, out_0, out_1, out_2):
         nc.scalar.activation(out=sin_half[:], in_=angles[:].rearrange("p t i -> p (t i)"), func=SIN, scale=0.5)
         nc.scalar.activation(out=sin_quarter[:], in_=angles[:].rearrange("p t i -> p (t i)"), func=SIN, scale=0.25)
 
-        square_half = tables.tile([P, n_angles], F32)
-        square_quarter = tables.tile([P, n_angles], F32)
-        cos_half = tables.tile([P, n_angles], F32)
-        half_sin = tables.tile([P, n_angles], F32)
-        nc.vector.tensor_tensor(out=square_half[:], in0=sin_half[:], in1=sin_half[:], op=MULT)
-        nc.vector.tensor_tensor(out=square_quarter[:], in0=sin_quarter[:], in1=sin_quarter[:], op=MULT)
-        nc.vector.tensor_scalar(
-            out=cos_half[:], in0=square_quarter[:], scalar1=-2.0, scalar2=1.0, op0=MULT, op1=ADD
-        )
-        nc.vector.tensor_tensor(out=half_sin[:], in0=sin_half[:], in1=cos_half[:], op=MULT)
-        from_even = tables.tile([P, POSITION_TILES, PAIRS, 2], F32)
-        from_odd = tables.tile([P, POSITION_TILES, PAIRS, 2], F32)
-        even_factors = from_even[:].rearrange("p t i j -> p (t i) j")
-        odd_factors = from_odd[:].rearrange("p t i j -> p (t i) j")
-        for cos_place in (even_factors[:, :, 0], odd_factors[:, :, 1]):
-            nc.vector.tensor_scalar(
-                out=cos_place, in0=square_half[:], scalar1=-2.0, scalar2=1.0, op0=MULT, op1=ADD
-            )
-        nc.vector.tensor_scalar_mul(out=even_factors[:, :, 1], in0=half_sin[:], scalar1=2.0)
-        nc.vector.tensor_scalar_mul(out=odd_factors[:, :, 0], in0=half_sin[:], scalar1=-2.0)
+        factors = tables.tile([P, POSITION_TILES, 3, PAIRS], F32)
+        sin_square = tables.tile([P, n_angles], F32)
+        quarter_square = tables.tile([P, n_angles], F32)
+
+        def by_tile(table):
+            return table[:].rearrange("p (t i) -> p t i", i=PAIRS)
+
+        def times(out, in0, scalar, in1, op0):
+            nc.vector.scalar_tensor_tensor(out=out, in0=in0, scalar=scalar, in1=in1, op0=op0, op1=MULT)
+
+        times(quarter_square[:], sin_quarter[:], -4.0, sin_quarter[:], MULT)
+        times(factors[:, :, 2, :], by_tile(quarter_square), 2.0, by_tile(sin_half), ADD)
+        nc.vector.tensor_scalar_mul(out=factors[:, :, 0, :], in0=factors[:, :, 2, :], scalar1=-1.0)
+        times(sin_square[:], sin_half[:], -2.0, sin_half[:], MULT)
+        nc.vector.tensor_scalar_add(out=factors[:, :, 1, :], in0=by_tile(sin_square), scalar1=1.0)
 
         x_codes = [quantised.tile([P, 2, PASSES, P], U32, name="x_codes%d" % j, align_bytes=256) for j in range(X_PAIRS)]
         x_scales = [quantised.tile([P, 2, PASSES, P], U8, name="x_scales%d" % j, align_bytes=256) for j in range(X_PAIRS)]
         w_codes = [quantised.tile([P, PASSES, W_PAIR], U32, name="w_codes%d" % i, align_bytes=256) for i in range(W_PAIRS)]
         w_scales = [quantised.tile([P, PASSES, W_PAIR], U8, name="w_scales%d" % i, align_bytes=256) for i in range(W_PAIRS)]
 
+        def transpose_two_passes(rows, first_pass, place):
+            words = rows[:].bitcast(F32)
+            bank = banks.tile([P, 2, 2, P], F32, tag="turned", name="bank")
+            for g in range(2):
+                for u in range(2):
+                    first_word = (2 * (first_pass + g) + u) * P
+                    nc.tensor.transpose(bank[:, g, u, :], words[:, first_word : first_word + P], identity[:])
+            nc.scalar.copy(out=place, in_=bank[:].rearrange("p g u r -> p g r u"))
+
+        def prepare_half(step, half):
+            kind, index = GROUPS[step]
+            passes = slice(2 * half, 2 * half + 2)
+            grouped = stage.tile([P, FEATURES], BF16, align_bytes=64, name="grouped_half")
+            words_out = grouped[:].bitcast(F32)
+            if kind == "w":
+                by_block = words_out.rearrange("p (g b r u) -> p b g r u", b=2, g=2, u=2)
+            else:
+                by_block = words_out.rearrange("p (b g r u) -> p b g r u", b=2, g=2, u=2)
+            for b in range(2):
+                transpose_two_passes(raw_tiles[step][b], 2 * half, by_block[:, b])
+                if kind == "x":
+                    nc.vector.quantize_mx(
+                        out=x_codes[index][:, b, passes].rearrange("p g r -> p (g r)").bitcast(FP8X4),
+                        scales=x_scales[index][:, b, passes].rearrange("p g r -> p (g r)"),
+                        in_=grouped[:, b * FEATURES // 2 : (b + 1) * FEATURES // 2],
+                    )
+            if kind == "w":
+                nc.vector.quantize_mx(
+                    out=w_codes[index][:, passes].rearrange("p g r -> p (g r)").bitcast(FP8X4),
+                    scales=w_scales[index][:, passes].rearrange("p g r -> p (g r)"),
+                    in_=grouped[:],
+                )
+
         def transpose_group(step):
             kind, index = GROUPS[step]
             grouped = stage.tile([P, 2 * PASSES * P * PACK], BF16, align_bytes=64)
             words_out = grouped[:].bitcast(F32)
             for b in range(2):
-                words = raw_tiles[step][b][:].bitcast(F32)
                 for first_pass in range(0, PASSES, 2):
-                    bank = banks.tile([P, 2, 2, P], F32, tag="turned")
-                    for g in range(2):
-                        for u in range(2):
-                            first_word = (2 * (first_pass + g) + u) * P
-                            nc.tensor.transpose(bank[:, g, u, :], words[:, first_word : first_word + P], identity[:])
                     if kind == "x":
                         place = words_out.rearrange("p (b g r u) -> p b g r u", b=2, g=PASSES, u=2)[:, b]
                     else:
                         place = words_out.rearrange("p (g b r u) -> p b g r u", b=2, g=PASSES, u=2)[:, b]
-                    nc.scalar.copy(
-                        out=place[:, first_pass : first_pass + 2, :, :],
-                        in_=bank[:].rearrange("p g u r -> p g r u"),
+                    transpose_two_passes(
+                        raw_tiles[step][b], first_pass, place[:, first_pass : first_pass + 2, :, :]
                     )
             return grouped
 
@@ -165,31 +189,39 @@ def tile_attention_pa_kernel(tc, x, freqs, wq, wk, wv, out_0, out_1, out_2):
                 place = q_view[:, positions, (w_index - 1) * W_PAIR : w_index * W_PAIR]
             return place.rearrange("b p n -> p b n")
 
+        def rotate(total, x_index, columns, adder):
+            heads = columns // HEAD
+            features = total.rearrange("p (h i e) -> p h i e", h=heads, e=2)
+            parts = []
+            for e in range(2):
+                planes = factors[:, x_index, 1 - e : 3 - e, :].rearrange("p j i -> p i j")
+                part = parts_pool.tile([P, columns], F32, name="part%d" % e)
+                nc.vector.tensor_tensor(
+                    out=part[:].rearrange("p (h i j) -> p h i j", h=heads, j=2),
+                    in0=features[:, :, :, e : e + 1].to_broadcast([P, heads, PAIRS, 2]),
+                    in1=planes.unsqueeze(1).to_broadcast([P, heads, PAIRS, 2]),
+                    op=MULT,
+                )
+                parts.append(part)
+            rows = results.tile([P, columns], F32, name="rows")
+            adder.tensor_tensor(out=rows[:], in0=parts[0][:], in1=parts[1][:], op=ADD)
+            return rows
+
         def finish(unit, total, adder):
             w_index, x_index = unit
             flat = total[:].rearrange("p b n -> p (b n)")
-            rows = results.tile([P, 2 * W_PAIR], F32, name="rows")
             if w_index == W_PAIRS - 1:
+                rows = results.tile([P, 2 * W_PAIR], F32, name="rows")
                 nc.scalar.copy(out=rows[:], in_=flat)
+                queue = nc.scalar
             else:
-                heads = 2 * W_PAIR // HEAD
-                features = flat.rearrange("p (h i e) -> p h i e", h=heads, e=2)
-                parts = []
-                for e, factors in ((0, from_even), (1, from_odd)):
-                    part = parts_pool.tile([P, 2 * W_PAIR], F32, name="part%d" % e)
-                    nc.vector.tensor_tensor(
-                        out=part[:].rearrange("p (h i j) -> p h i j", h=heads, j=2),
-                        in0=features[:, :, :, e : e + 1].to_broadcast([P, heads, PAIRS, 2]),
-                        in1=factors[:, x_index, :, :].unsqueeze(1).to_broadcast([P, heads, PAIRS, 2]),
-                        op=MULT,
-                    )
-                    parts.append(part)
-                adder.tensor_tensor(out=rows[:], in0=parts[0][:], in1=parts[1][:], op=ADD)
-            nc.sync.dma_start(out=place_of(unit), in_=rows[:].rearrange("p (b n) -> p b n", b=2))
+                rows = rotate(flat, x_index, 2 * W_PAIR, adder)
+                queue = nc.sync
+            queue.dma_start(out=place_of(unit), in_=rows[:].rearrange("p (b n) -> p b n", b=2))
 
-        def multiply(out, unit, b):
+        def multiply(out, unit, b, passes=range(PASSES)):
             w_index, x_index = unit
-            for g in range(PASSES):
+            for g in passes:
                 nc.tensor.matmul_mx(
                     out=out,
                     lhsT=x_codes[x_index][:, b, g, :].bitcast(FP8X4),
@@ -206,19 +238,28 @@ def tile_attention_pa_kernel(tc, x, freqs, wq, wk, wv, out_0, out_1, out_2):
                 multiply(total[:], unit, b)
                 rows = results.tile([P, W_PAIR], F32, name="half_rows")
                 nc.scalar.copy(out=rows[:], in_=total[:])
-                nc.sync.dma_start(out=place_of(unit)[:, b, :], in_=rows[:])
+                nc.scalar.dma_start(out=place_of(unit)[:, b, :], in_=rows[:])
 
-        for step in range(2):
-            quantise_group(step, transpose_group(step))
-        for step in range(1, LAST - 1):
+        prepare_half(0, 0)
+        prepare_half(1, 0)
+        prepare_half(0, 1)
+        first_unit = units_of(1)[0]
+        open_totals = [banks.tile([P, W_PAIR], F32, tag="sums", name="open%d" % b) for b in range(2)]
+        for b in range(2):
+            multiply(open_totals[b][:], first_unit, b, range(2))
+        prepare_half(1, 1)
+        quantise_group(2, transpose_group(2))
+        for b in range(2):
+            multiply(open_totals[b][:], first_unit, b, range(2, PASSES))
+        for b in range(2):
+            rows = rotate(open_totals[b][:], first_unit[1], W_PAIR, nc.gpsimd)
+            nc.sync.dma_start(out=place_of(first_unit)[:, b, :], in_=rows[:])
+        for step in range(2, LAST - 1):
             units = units_of(step)
             grouped = transpose_group(step + 1)
-            early = units[:1] if len(units) > 1 else []
-            for unit in early:
-                finish(unit, project(unit, "sums"), nc.gpsimd)
             quantise_group(step + 1, grouped)
-            for unit in units[len(early) :]:
-                finish(unit, project(unit, "sums"), nc.gpsimd if early else nc.vector)
+            for unit in units:
+                finish(unit, project(unit, "sums"), nc.gpsimd)
         quantise_group(LAST, transpose_group(LAST))
         q_units = units_of(LAST - 1)
         v_units = units_of(LAST)

@@ -39,23 +39,19 @@ def units_of(step):
 
 def tile_attention_pa_kernel(tc, x, freqs, wq, wk, wv, out_0, out_1, out_2):
     nc = tc.nc
-    x_rows = x.rearrange("b s k d -> (b s k) d")
+    x_rows = x.rearrange("b s k d -> b (s k) d")
     angle_rows = freqs.rearrange("s k i -> (s k) i")
     q_view = out_0.rearrange("b s k h d -> b (s k) (h d)")
     k_view = out_1.rearrange("b s k h d -> b (s k) (h d)")
     v_view = out_2.rearrange("b s k h d -> b (s k) (h d)")
 
-    w_block_rows = (
-        [wk[r : r + P, :] for r in range(0, W_PAIR, P)]
-        + [wq[r : r + P, :] for r in range(0, 4 * W_PAIR, P)]
-        + [wv[r : r + P, :] for r in range(0, W_PAIR, P)]
-    )
+    w_pair_rows = [wk] + [wq[r : r + W_PAIR, :] for r in range(0, 4 * W_PAIR, W_PAIR)] + [wv]
 
-    def block_rows(group):
+    def pair_rows(group):
         kind, index = group
         if kind == "w":
-            return w_block_rows[2 * index : 2 * index + 2]
-        return [x_rows[t * P : (t + 1) * P, :] for t in (index, index + X_PAIRS)]
+            return w_pair_rows[index].rearrange("(b p) d -> p b d", b=2)
+        return x_rows[:, index * P : (index + 1) * P, :].rearrange("b p d -> p b d")
 
     with ExitStack() as ctx:
         ctx.enter_context(tc.manual_schedule())
@@ -65,20 +61,22 @@ def tile_attention_pa_kernel(tc, x, freqs, wq, wk, wv, out_0, out_1, out_2):
         quantised = ctx.enter_context(tc.tile_pool(name="quantised", bufs=1))
         stage = ctx.enter_context(tc.tile_pool(name="stage", bufs=3))
         parts_pool = ctx.enter_context(tc.tile_pool(name="parts", bufs=6))
-        results = ctx.enter_context(tc.tile_pool(name="results", bufs=10))
+        results = ctx.enter_context(tc.tile_pool(name="results", bufs=16))
+        small_results = ctx.enter_context(tc.tile_pool(name="small_results", bufs=3))
         banks = ctx.enter_context(tc.psum_pool(name="banks", bufs=4))
 
-        raw_tiles = [
-            [raw.tile([P, FEATURES], BF16, name="raw%d_%d" % (s, b)) for b in range(2)] for s in range(len(GROUPS))
-        ]
+        raw_halves = {}
         for half in range(2):
             columns = slice(half * FEATURES // 2, (half + 1) * FEATURES // 2)
             for step in range(2):
-                for b, rows in enumerate(block_rows(GROUPS[step])):
-                    nc.sync.dma_start(out=raw_tiles[step][b][:, columns], in_=rows[:, columns])
+                raw_half = raw.tile([P, 2, FEATURES // 2], BF16, name="raw_half%d_%d" % (step, half))
+                nc.sync.dma_start(out=raw_half[:], in_=pair_rows(GROUPS[step])[:, :, columns])
+                raw_halves[step, half] = raw_half
+        raw_pairs = {}
         for step in range(2, len(GROUPS)):
-            for b, rows in enumerate(block_rows(GROUPS[step])):
-                nc.sync.dma_start(out=raw_tiles[step][b][:], in_=rows)
+            raw_pair = raw.tile([P, 2, FEATURES], BF16, name="raw%d" % step)
+            nc.sync.dma_start(out=raw_pair[:], in_=pair_rows(GROUPS[step]))
+            raw_pairs[step] = raw_pair
 
         angles = tables.tile([P, POSITION_TILES, PAIRS], BF16)
         nc.scalar.dma_start(out=angles[:], in_=angle_rows.rearrange("(t p) i -> p t i", p=P))
@@ -113,7 +111,7 @@ def tile_attention_pa_kernel(tc, x, freqs, wq, wk, wv, out_0, out_1, out_2):
         w_scales = [quantised.tile([P, PASSES, W_PAIR], U8, name="w_scales%d" % i, align_bytes=256) for i in range(W_PAIRS)]
 
         def transpose_two_passes(rows, first_pass, place):
-            words = rows[:].bitcast(F32)
+            words = rows.bitcast(F32)
             bank = banks.tile([P, 2, 2, P], F32, tag="turned", name="bank")
             for g in range(2):
                 for u in range(2):
@@ -131,7 +129,7 @@ def tile_attention_pa_kernel(tc, x, freqs, wq, wk, wv, out_0, out_1, out_2):
             else:
                 by_block = words_out.rearrange("p (b g r u) -> p b g r u", b=2, g=2, u=2)
             for b in range(2):
-                transpose_two_passes(raw_tiles[step][b], 2 * half, by_block[:, b])
+                transpose_two_passes(raw_halves[step, half][:, b, :], 0, by_block[:, b])
                 if kind == "x":
                     nc.vector.quantize_mx(
                         out=x_codes[index][:, b, passes].rearrange("p g r -> p (g r)").bitcast(FP8X4),
@@ -156,7 +154,7 @@ def tile_attention_pa_kernel(tc, x, freqs, wq, wk, wv, out_0, out_1, out_2):
                     else:
                         place = words_out.rearrange("p (g b r u) -> p b g r u", b=2, g=PASSES, u=2)[:, b]
                     transpose_two_passes(
-                        raw_tiles[step][b], first_pass, place[:, first_pass : first_pass + 2, :, :]
+                        raw_pairs[step][:, b, :], first_pass, place[:, first_pass : first_pass + 2, :, :]
                     )
             return grouped
 
@@ -219,26 +217,33 @@ def tile_attention_pa_kernel(tc, x, freqs, wq, wk, wv, out_0, out_1, out_2):
                 queue = nc.sync
             queue.dma_start(out=place_of(unit), in_=rows[:].rearrange("p (b n) -> p b n", b=2))
 
-        def multiply(out, unit, b, passes=range(PASSES)):
+        def multiply(out, unit, b, passes=range(PASSES), rows=slice(0, W_PAIR)):
             w_index, x_index = unit
             for g in passes:
                 nc.tensor.matmul_mx(
                     out=out,
                     lhsT=x_codes[x_index][:, b, g, :].bitcast(FP8X4),
                     lhsT_scale=x_scales[x_index][:, b, g, :],
-                    rhs=w_codes[w_index][:, g, :].bitcast(FP8X4),
-                    rhs_scale=w_scales[w_index][:, g, :],
+                    rhs=w_codes[w_index][:, g, rows].bitcast(FP8X4),
+                    rhs_scale=w_scales[w_index][:, g, rows],
                     start=(g == 0),
                     stop=(g == PASSES - 1),
                 )
 
         def last_v_unit(unit):
-            for b in range(2):
-                total = banks.tile([P, W_PAIR], F32, tag=("sums", "turned")[b], name="half_total")
-                multiply(total[:], unit, b)
-                rows = results.tile([P, W_PAIR], F32, name="half_rows")
-                nc.scalar.copy(out=rows[:], in_=total[:])
-                nc.scalar.dma_start(out=place_of(unit)[:, b, :], in_=rows[:])
+            w_index, x_index = unit
+            pieces = ((0, 0, W_PAIR), (1, 0, P), (1, P, P))
+            for i, (b, first_row, width) in enumerate(pieces):
+                total = banks.tile([P, width], F32, tag=("sums", "turned")[i % 2], name="piece_total")
+                multiply(total[:], unit, b, rows=slice(first_row, first_row + width))
+                rows = small_results.tile([P, width], F32, name="piece_rows")
+                place = place_of(unit)[:, b, first_row : first_row + width]
+                if i % 2 == 0:
+                    nc.vector.tensor_copy(out=rows[:], in_=total[:])
+                    nc.sync.dma_start(out=place, in_=rows[:])
+                else:
+                    nc.scalar.copy(out=rows[:], in_=total[:])
+                    nc.scalar.dma_start(out=place, in_=rows[:])
 
         prepare_half(0, 0)
         prepare_half(1, 0)
@@ -263,7 +268,7 @@ def tile_attention_pa_kernel(tc, x, freqs, wq, wk, wv, out_0, out_1, out_2):
         quantise_group(LAST, transpose_group(LAST))
         q_units = units_of(LAST - 1)
         v_units = units_of(LAST)
-        order = q_units[:2] + v_units[:1] + q_units[2:] + v_units[1:-1]
+        order = q_units[:3] + v_units[:1] + q_units[3:] + v_units[1:-1]
         for i, unit in enumerate(order):
             adder = nc.vector if unit == q_units[-1] else nc.gpsimd
             finish(unit, project(unit, ("sums", "turned")[i % 2]), adder)

@@ -99,11 +99,12 @@ def tile_attention_pa_kernel(tc, x, freqs, wq, wk, wv, out_0, out_1, out_2):
         def times(out, in0, scalar, in1, op0):
             nc.vector.scalar_tensor_tensor(out=out, in0=in0, scalar=scalar, in1=in1, op0=op0, op1=MULT)
 
-        times(quarter_square[:], sin_quarter[:], -4.0, sin_quarter[:], MULT)
-        times(factors[:, :, 2, :], by_tile(quarter_square), 2.0, by_tile(sin_half), ADD)
-        nc.vector.tensor_scalar_mul(out=factors[:, :, 0, :], in0=factors[:, :, 2, :], scalar1=-1.0)
-        times(sin_square[:], sin_half[:], -2.0, sin_half[:], MULT)
-        nc.vector.tensor_scalar_add(out=factors[:, :, 1, :], in0=by_tile(sin_square), scalar1=1.0)
+        def make_factors():
+            times(quarter_square[:], sin_quarter[:], -4.0, sin_quarter[:], MULT)
+            times(factors[:, :, 2, :], by_tile(quarter_square), 2.0, by_tile(sin_half), ADD)
+            nc.vector.tensor_scalar_mul(out=factors[:, :, 0, :], in0=factors[:, :, 2, :], scalar1=-1.0)
+            times(sin_square[:], sin_half[:], -2.0, sin_half[:], MULT)
+            nc.vector.tensor_scalar_add(out=factors[:, :, 1, :], in0=by_tile(sin_square), scalar1=1.0)
 
         x_codes = [quantised.tile([P, 2, PASSES, P], U32, name="x_codes%d" % j, align_bytes=256) for j in range(X_PAIRS)]
         x_scales = [quantised.tile([P, 2, PASSES, P], U8, name="x_scales%d" % j, align_bytes=256) for j in range(X_PAIRS)]
@@ -147,28 +148,33 @@ def tile_attention_pa_kernel(tc, x, freqs, wq, wk, wv, out_0, out_1, out_2):
             kind, index = GROUPS[step]
             grouped = stage.tile([P, 2 * PASSES * P * PACK], BF16, align_bytes=64)
             words_out = grouped[:].bitcast(F32)
-            for b in range(2):
-                for first_pass in range(0, PASSES, 2):
-                    if kind == "x":
-                        place = words_out.rearrange("p (b g r u) -> p b g r u", b=2, g=PASSES, u=2)[:, b]
-                    else:
-                        place = words_out.rearrange("p (g b r u) -> p b g r u", b=2, g=PASSES, u=2)[:, b]
-                    transpose_two_passes(
-                        raw_pairs[step][:, b, :], first_pass, place[:, first_pass : first_pass + 2, :, :]
-                    )
+            if kind == "x":
+                by_block = words_out.rearrange("p (b g r u) -> p b g r u", b=2, g=PASSES, u=2)
+                order = [(b, half) for b in range(2) for half in range(2)]
+            else:
+                by_block = words_out.rearrange("p (g b r u) -> p b g r u", b=2, g=PASSES, u=2)
+                order = [(b, half) for half in range(2) for b in range(2)]
+            for b, half in order:
+                transpose_two_passes(raw_pairs[step][:, b, :], 2 * half, by_block[:, b, 2 * half : 2 * half + 2])
             return grouped
 
         def quantise_group(step, grouped):
             kind, index = GROUPS[step]
-            for half in range(2):
-                values = grouped[:, half * FEATURES : (half + 1) * FEATURES]
+            pieces = [(b, half) for b in range(2) for half in range(2)] if kind == "x" else [(0, 0), (0, 1)]
+            width = 2 * FEATURES // len(pieces)
+            for i, (b, half) in enumerate(pieces):
+                passes = slice(2 * half, 2 * half + 2)
                 if kind == "x":
-                    codes = x_codes[index][:, half].rearrange("p g r -> p (g r)")
-                    scales = x_scales[index][:, half].rearrange("p g r -> p (g r)")
+                    codes = x_codes[index][:, b, passes]
+                    scales = x_scales[index][:, b, passes]
                 else:
-                    codes = w_codes[index][:, 2 * half : 2 * half + 2].rearrange("p g r -> p (g r)")
-                    scales = w_scales[index][:, 2 * half : 2 * half + 2].rearrange("p g r -> p (g r)")
-                nc.vector.quantize_mx(out=codes.bitcast(FP8X4), scales=scales, in_=values)
+                    codes = w_codes[index][:, passes]
+                    scales = w_scales[index][:, passes]
+                nc.vector.quantize_mx(
+                    out=codes.rearrange("p g r -> p (g r)").bitcast(FP8X4),
+                    scales=scales.rearrange("p g r -> p (g r)"),
+                    in_=grouped[:, i * width : (i + 1) * width],
+                )
 
         def project(unit, tag):
             total = banks.tile([P, 2, W_PAIR], F32, tag=tag)
@@ -247,6 +253,7 @@ def tile_attention_pa_kernel(tc, x, freqs, wq, wk, wv, out_0, out_1, out_2):
 
         prepare_half(0, 0)
         prepare_half(1, 0)
+        make_factors()
         prepare_half(0, 1)
         first_unit = units_of(1)[0]
         open_totals = [banks.tile([P, W_PAIR], F32, tag="sums", name="open%d" % b) for b in range(2)]

from contextlib import ExitStack

import concourse.mybir as mybir
from concourse.masks import make_identity

F32 = mybir.dt.float32
BF16 = mybir.dt.bfloat16
U32 = mybir.dt.uint32
U8 = mybir.dt.uint8
FP8X4 = mybir.dt.float8_e4m3fn_x4
MULT = mybir.AluOpType.mult
ADD = mybir.AluOpType.add
SIN = mybir.ActivationFunctionType.Sin

P = 128
PACK = 4
K_PASS = P * PACK
FEATURES = 2048
PASSES = FEATURES // K_PASS
TOKENS = 2 * 16 * 32
POSITION_TILES = 16 * 32 // P
HEAD = 128
PAIRS = HEAD // 2
W_PAIR = 2 * P
W_PAIRS = 6
X_PAIRS = POSITION_TILES

FLOPS = 2 * TOKENS * FEATURES * W_PAIRS * W_PAIR

GROUPS = (("w", 0), ("x", 0), ("w", 1), ("x", 1), ("w", 2), ("x", 2), ("w", 3), ("x", 3), ("w", 4), ("w", 5))
LAST = len(GROUPS) - 1


def units_of(step):
    kind, index = GROUPS[step]
    seen = [i for k, i in GROUPS[:step] if k != kind]
    return [(i, index) if kind == "x" else (index, i) for i in seen]


def tile_attention_pa_kernel(tc, x, freqs, wq, wk, wv, out_0, out_1, out_2):
    nc = tc.nc
    x_rows = x.rearrange("b s k d -> b (s k) d")
    angle_rows = freqs.rearrange("s k i -> (s k) i")
    q_view = out_0.rearrange("b s k h d -> b (s k) (h d)")
    k_view = out_1.rearrange("b s k h d -> b (s k) (h d)")
    v_view = out_2.rearrange("b s k h d -> b (s k) (h d)")

    w_pair_rows = [wk] + [wq[r : r + W_PAIR, :] for r in range(0, 4 * W_PAIR, W_PAIR)] + [wv]

    def pair_rows(group):
        kind, index = group
        if kind == "w":
            return w_pair_rows[index].rearrange("(b p) d -> p b d", b=2)
        return x_rows[:, index * P : (index + 1) * P, :].rearrange("b p d -> p b d")

    with ExitStack() as ctx:
        ctx.enter_context(tc.manual_schedule())

        raw = ctx.enter_context(tc.tile_pool(name="raw", bufs=1))
        tables = ctx.enter_context(tc.tile_pool(name="tables", bufs=1))
        quantised = ctx.enter_context(tc.tile_pool(name="quantised", bufs=1))
        stage = ctx.enter_context(tc.tile_pool(name="stage", bufs=3))
        parts_pool = ctx.enter_context(tc.tile_pool(name="parts", bufs=6))
        results = ctx.enter_context(tc.tile_pool(name="results", bufs=16))
        small_results = ctx.enter_context(tc.tile_pool(name="small_results", bufs=3))
        banks = ctx.enter_context(tc.psum_pool(name="banks", bufs=4))

        raw_halves = {}
        for half in range(2):
            columns = slice(half * FEATURES // 2, (half + 1) * FEATURES // 2)
            for step in range(2):
                raw_half = raw.tile([P, 2, FEATURES // 2], BF16, name="raw_half%d_%d" % (step, half))
                nc.sync.dma_start(out=raw_half[:], in_=pair_rows(GROUPS[step])[:, :, columns])
                raw_halves[step, half] = raw_half
        raw_pairs = {}
        for step in range(2, len(GROUPS)):
            raw_pair = raw.tile([P, 2, FEATURES], BF16, name="raw%d" % step)
            nc.sync.dma_start(out=raw_pair[:], in_=pair_rows(GROUPS[step]))
            raw_pairs[step] = raw_pair

        angles = tables.tile([P, POSITION_TILES, PAIRS], BF16)
        nc.scalar.dma_start(out=angles[:], in_=angle_rows.rearrange("(t p) i -> p t i", p=P))
        identity = tables.tile([P, P], F32)
        make_identity(nc, identity[:])

        n_angles = POSITION_TILES * PAIRS
        sin_half = tables.tile([P, n_angles], F32)
        sin_quarter = tables.tile([P, n_angles], F32)
        nc.scalar.activation(out=sin_half[:], in_=angles[:].rearrange("p t i -> p (t i)"), func=SIN, scale=0.5)
        nc.scalar.activation(out=sin_quarter[:], in_=angles[:].rearrange("p t i -> p (t i)"), func=SIN, scale=0.25)

        factors = tables.tile([P, POSITION_TILES, 3, PAIRS], F32)
        sin_square = tables.tile([P, n_angles], F32)
        quarter_square = tables.tile([P, n_angles], F32)

        def by_tile(table):
            return table[:].rearrange("p (t i) -> p t i", i=PAIRS)

        def times(out, in0, scalar, in1, op0):
            nc.vector.scalar_tensor_tensor(out=out, in0=in0, scalar=scalar, in1=in1, op0=op0, op1=MULT)

        def make_factors():
            times(quarter_square[:], sin_quarter[:], -4.0, sin_quarter[:], MULT)
            times(factors[:, :, 2, :], by_tile(quarter_square), 2.0, by_tile(sin_half), ADD)
            nc.vector.tensor_scalar_mul(out=factors[:, :, 0, :], in0=factors[:, :, 2, :], scalar1=-1.0)
            times(sin_square[:], sin_half[:], -2.0, sin_half[:], MULT)
            nc.vector.tensor_scalar_add(out=factors[:, :, 1, :], in0=by_tile(sin_square), scalar1=1.0)

        x_codes = [quantised.tile([P, 2, PASSES, P], U32, name="x_codes%d" % j, align_bytes=256) for j in range(X_PAIRS)]
        x_scales = [quantised.tile([P, 2, PASSES, P], U8, name="x_scales%d" % j, align_bytes=256) for j in range(X_PAIRS)]
        w_codes = [quantised.tile([P, PASSES, W_PAIR], U32, name="w_codes%d" % i, align_bytes=256) for i in range(W_PAIRS)]
        w_scales = [quantised.tile([P, PASSES, W_PAIR], U8, name="w_scales%d" % i, align_bytes=256) for i in range(W_PAIRS)]

        def transpose_two_passes(rows, first_pass, place):
            words = rows.bitcast(F32)
            bank = banks.tile([P, 2, 2, P], F32, tag="turned", name="bank")
            for g in range(2):
                for u in range(2):
                    first_word = (2 * (first_pass + g) + u) * P
                    nc.tensor.transpose(bank[:, g, u, :], words[:, first_word : first_word + P], identity[:])
            nc.scalar.copy(out=place, in_=bank[:].rearrange("p g u r -> p g r u"))

        def prepare_half(step, half):
            kind, index = GROUPS[step]
            passes = slice(2 * half, 2 * half + 2)
            grouped = stage.tile([P, FEATURES], BF16, align_bytes=64, name="grouped_half")
            words_out = grouped[:].bitcast(F32)
            if kind == "w":
                by_block = words_out.rearrange("p (g b r u) -> p b g r u", b=2, g=2, u=2)
            else:
                by_block = words_out.rearrange("p (b g r u) -> p b g r u", b=2, g=2, u=2)
            for b in range(2):
                transpose_two_passes(raw_halves[step, half][:, b, :], 0, by_block[:, b])
                if kind == "x":
                    nc.vector.quantize_mx(
                        out=x_codes[index][:, b, passes].rearrange("p g r -> p (g r)").bitcast(FP8X4),
                        scales=x_scales[index][:, b, passes].rearrange("p g r -> p (g r)"),
                        in_=grouped[:, b * FEATURES // 2 : (b + 1) * FEATURES // 2],
                    )
            if kind == "w":
                nc.vector.quantize_mx(
                    out=w_codes[index][:, passes].rearrange("p g r -> p (g r)").bitcast(FP8X4),
                    scales=w_scales[index][:, passes].rearrange("p g r -> p (g r)"),
                    in_=grouped[:],
                )

        def transpose_group(step):
            kind, index = GROUPS[step]
            grouped = stage.tile([P, 2 * PASSES * P * PACK], BF16, align_bytes=64)
            words_out = grouped[:].bitcast(F32)
            if kind == "x":
                by_block = words_out.rearrange("p (b g r u) -> p b g r u", b=2, g=PASSES, u=2)
                order = [(b, half) for b in range(2) for half in range(2)]
            else:
                by_block = words_out.rearrange("p (g b r u) -> p b g r u", b=2, g=PASSES, u=2)
                order = [(b, half) for half in range(2) for b in range(2)]
            for b, half in order:
                transpose_two_passes(raw_pairs[step][:, b, :], 2 * half, by_block[:, b, 2 * half : 2 * half + 2])
            return grouped

        def quantise_group(step, grouped):
            kind, index = GROUPS[step]
            pieces = [(b, half) for b in range(2) for half in range(2)] if kind == "x" else [(0, 0), (0, 1)]
            width = 2 * FEATURES // len(pieces)
            for i, (b, half) in enumerate(pieces):
                passes = slice(2 * half, 2 * half + 2)
                if kind == "x":
                    codes = x_codes[index][:, b, passes]
                    scales = x_scales[index][:, b, passes]
                else:
                    codes = w_codes[index][:, passes]
                    scales = w_scales[index][:, passes]
                nc.vector.quantize_mx(
                    out=codes.rearrange("p g r -> p (g r)").bitcast(FP8X4),
                    scales=scales.rearrange("p g r -> p (g r)"),
                    in_=grouped[:, i * width : (i + 1) * width],
                )

        def project(unit, tag):
            total = banks.tile([P, 2, W_PAIR], F32, tag=tag)
            for b in range(2):
                multiply(total[:, b, :], unit, b)
            return total

        def place_of(unit):
            w_index, x_index = unit
            positions = slice(x_index * P, (x_index + 1) * P)
            if w_index == 0:
                place = k_view[:, positions, :]
            elif w_index == W_PAIRS - 1:
                place = v_view[:, positions, :]
            else:
                place = q_view[:, positions, (w_index - 1) * W_PAIR : w_index * W_PAIR]
            return place.rearrange("b p n -> p b n")

        def rotate(total, x_index, columns, adder):
            heads = columns // HEAD
            features = total.rearrange("p (h i e) -> p h i e", h=heads, e=2)
            parts = []
            for e in range(2):
                planes = factors[:, x_index, 1 - e : 3 - e, :].rearrange("p j i -> p i j")
                part = parts_pool.tile([P, columns], F32, name="part%d" % e)
                nc.vector.tensor_tensor(
                    out=part[:].rearrange("p (h i j) -> p h i j", h=heads, j=2),
                    in0=features[:, :, :, e : e + 1].to_broadcast([P, heads, PAIRS, 2]),
                    in1=planes.unsqueeze(1).to_broadcast([P, heads, PAIRS, 2]),
                    op=MULT,
                )
                parts.append(part)
            rows = results.tile([P, columns], F32, name="rows")
            adder.tensor_tensor(out=rows[:], in0=parts[0][:], in1=parts[1][:], op=ADD)
            return rows

        def finish(unit, total, adder):
            w_index, x_index = unit
            flat = total[:].rearrange("p b n -> p (b n)")
            if w_index == W_PAIRS - 1:
                rows = results.tile([P, 2 * W_PAIR], F32, name="rows")
                nc.scalar.copy(out=rows[:], in_=flat)
                queue = nc.scalar
            else:
                rows = rotate(flat, x_index, 2 * W_PAIR, adder)
                queue = nc.sync
            queue.dma_start(out=place_of(unit), in_=rows[:].rearrange("p (b n) -> p b n", b=2))

        def multiply(out, unit, b, passes=range(PASSES), rows=slice(0, W_PAIR)):
            w_index, x_index = unit
            for g in passes:
                nc.tensor.matmul_mx(
                    out=out,
                    lhsT=x_codes[x_index][:, b, g, :].bitcast(FP8X4),
                    lhsT_scale=x_scales[x_index][:, b, g, :],
                    rhs=w_codes[w_index][:, g, rows].bitcast(FP8X4),
                    rhs_scale=w_scales[w_index][:, g, rows],
                    start=(g == 0),
                    stop=(g == PASSES - 1),
                )

        def last_v_unit(unit):
            w_index, x_index = unit
            pieces = ((0, 0, W_PAIR), (1, 0, P), (1, P, P))
            for i, (b, first_row, width) in enumerate(pieces):
                total = banks.tile([P, width], F32, tag=("sums", "turned")[i % 2], name="piece_total")
                multiply(total[:], unit, b, rows=slice(first_row, first_row + width))
                rows = small_results.tile([P, width], F32, name="piece_rows")
                place = place_of(unit)[:, b, first_row : first_row + width]
                if i % 2 == 0:
                    nc.vector.tensor_copy(out=rows[:], in_=total[:])
                    nc.sync.dma_start(out=place, in_=rows[:])
                else:
                    nc.scalar.copy(out=rows[:], in_=total[:])
                    nc.scalar.dma_start(out=place, in_=rows[:])

        prepare_half(0, 0)
        prepare_half(1, 0)
        make_factors()
        prepare_half(0, 1)
        first_unit = units_of(1)[0]
        open_totals = [banks.tile([P, W_PAIR], F32, tag="sums", name="open%d" % b) for b in range(2)]
        for b in range(2):
            multiply(open_totals[b][:], first_unit, b, range(2))
        prepare_half(1, 1)
        quantise_group(2, transpose_group(2))
        for b in range(2):
            multiply(open_totals[b][:], first_unit, b, range(2, PASSES))
        for b in range(2):
            rows = rotate(open_totals[b][:], first_unit[1], W_PAIR, nc.gpsimd)
            nc.sync.dma_start(out=place_of(first_unit)[:, b, :], in_=rows[:])
        for step in range(2, LAST - 1):
            units = units_of(step)
            grouped = transpose_group(step + 1)
            quantise_group(step + 1, grouped)
            for unit in units:
                finish(unit, project(unit, "sums"), nc.gpsimd)
        quantise_group(LAST, transpose_group(LAST))
        q_units = units_of(LAST - 1)
        v_units = units_of(LAST)
        order = q_units[:3] + v_units[:1] + q_units[3:] + v_units[1:-1]
        for i, unit in enumerate(order):
            adder = nc.vector if unit == q_units[-1] else nc.gpsimd
            finish(unit, project(unit, ("sums", "turned")[i % 2]), adder)
        last_v_unit(v_units[-1])
